import numpy as np
import ml_dtypes


def mxq(x, axis, fmt="e4m3"):
    dtype, down = {"e4m3": (ml_dtypes.float8_e4m3fn, 7), "e5m2": (ml_dtypes.float8_e5m2, 14)}[fmt]
    v = np.moveaxis(np.asarray(x, np.float32).astype(ml_dtypes.bfloat16).astype(np.float64), axis, -1)
    blocks = v.reshape(v.shape[:-1] + (-1, 32))
    amax = np.abs(blocks).max(-1, keepdims=True)
    byte = np.maximum(np.where(amax > 0, np.frexp(amax)[1] - 1 + 127, 0) - down, 1)
    scale = np.exp2(byte - 127.0)
    codes = (blocks / scale).astype(np.float32).astype(dtype).astype(np.float64)
    return np.moveaxis((codes * scale).reshape(v.shape), -1, axis)


WIDE = False


def mx_kscale(k):
    if not WIDE:
        return np.ones(k)
    levels = np.array([10, -10, 5, -5, 0])
    if k % 512:
        return np.exp2(np.random.permutation(np.resize(levels, k // 32))).repeat(32)
    a = np.empty((k // 512, 16))
    for p in range(k // 512):
        a[p, :8] = np.random.permutation(np.resize(levels, 8))
        for g in range(8):
            far = levels[np.abs(levels - a[p, g]) >= 10]
            a[p, g + 8] = far[np.random.randint(len(far))]
    return np.exp2(a.ravel()).repeat(32)


BF16 = ml_dtypes.bfloat16


def bf(x):
    return np.asarray(x, np.float32).astype(BF16)


def f64(x):
    return np.asarray(x).astype(np.float64)


BATCH, ROWS, COLS, IN_DIM, OUT_DIM = 2, 64, 64, 512, 512
N = ROWS * COLS
EPS_BN = 1e-5
EPS_DEG = 1e-5


def _stencil9(x):
    R, C = x.shape[-3], x.shape[-2]
    pad = [(0, 0)] * (x.ndim - 3) + [(1, 1), (1, 1), (0, 0)]
    xp = np.pad(x, pad)
    out = np.zeros_like(x)
    for di in range(3):
        for dj in range(3):
            out = out + xp[..., di:di + R, dj:dj + C, :]
    return out


def _deg_inv_sqrt(rows, cols):
    D = _stencil9(np.ones((rows, cols, 1)))[..., 0]
    return (D + EPS_DEG) ** -0.5


def setup_inputs():
    s = mx_kscale(IN_DIM)
    mu = 0.5 * np.random.standard_normal(IN_DIM)
    bound = np.sqrt(6.0 / IN_DIM)
    return {"H": bf((np.random.standard_normal((BATCH, N, IN_DIM)) + mu) * s),
            "W": bf(np.random.uniform(-bound, bound, (IN_DIM, OUT_DIM)) / s[:, None]),
            "gamma": bf(1.0 + 0.1 * np.random.standard_normal(OUT_DIM)),
            "beta": bf(0.2 * np.random.standard_normal(OUT_DIM))}


def core(H, W, gamma, beta):
    B, n_nodes, _ = H.shape
    Ht = mxq(f64(H), 2, "e4m3") @ mxq(f64(W), 0, "e4m3")
    mean = Ht.mean(axis=(0, 1))
    var = Ht.var(axis=(0, 1))
    Ht = (Ht - mean) * (1.0 / np.sqrt(var + EPS_BN)) * f64(gamma) + f64(beta)
    Ht = np.maximum(Ht, 0.0)
    d = _deg_inv_sqrt(ROWS, COLS)[None, :, :, None]
    Hg = Ht.reshape(B, ROWS, COLS, OUT_DIM)
    Hagg = d * _stencil9(Hg * d)
    return Hagg.reshape(B, n_nodes, OUT_DIM)


def e4m3fn_bytes(y):
    return np.clip(np.asarray(y, np.float64), -448.0, 448.0).astype(np.float32).astype(ml_dtypes.float8_e4m3fn).view(np.uint8)


Y_SCALE = 530.0


def reference(H, W, gamma, beta):
    out = core(H, W, gamma, beta)
    return out, e4m3fn_bytes(out * Y_SCALE)

@@ -1,0 +1,347 @@
+from contextlib import ExitStack
+
+import concourse.masks as masks
+import concourse.mybir as mybir
+
+F32 = mybir.dt.float32
+BF16 = mybir.dt.bfloat16
+U32 = mybir.dt.uint32
+U8 = mybir.dt.uint8
+FP8X4 = mybir.dt.float8_e4m3fn_x4
+FP8 = mybir.dt.float8_e4m3fn
+ALU = mybir.AluOpType
+ACT = mybir.ActivationFunctionType
+
+BATCH, NODES, K, FEAT = 2, 4096, 512, 512
+FLOPS = 2 * BATCH * NODES * K * FEAT
+
+P = 128
+J = NODES // P
+CH = 4
+NCH = J // CH
+NQ = BATCH * NCH
+FT = FEAT // P
+WIN = 130
+ZW = 5 * WIN
+Z0 = 4
+NZ = 3
+LOOK = 6
+
+EPS_BN = 1e-5
+EPS_DEG = 1e-5
+D9 = (9.0 + EPS_DEG) ** -0.5
+D6 = (6.0 + EPS_DEG) ** -0.5
+D4 = (4.0 + EPS_DEG) ** -0.5
+R69 = D6 / D9
+R46 = D4 / D6
+RC = D4 * D9 / (D6 * D6)
+Y_SCALE = 530.0
+VCAST = 1
+
+
+def tile_graphconvolutionbatch_kernel(tc, H, W, gamma, beta, out_0, out_1):
+    nc = tc.nc
+    with ExitStack() as ctx:
+        const = ctx.enter_context(tc.tile_pool(name="const", bufs=1))
+        hpool = ctx.enter_context(tc.tile_pool(name="hpool", bufs=8))
+        gpool = ctx.enter_context(tc.tile_pool(name="gpool", bufs=3))
+        work = ctx.enter_context(tc.tile_pool(name="work", bufs=3))
+        keep2 = ctx.enter_context(tc.tile_pool(name="keep2", bufs=2))
+        psY = ctx.enter_context(tc.psum_pool(name="psY", bufs=4))
+        psT = ctx.enter_context(tc.psum_pool(name="psT", bufs=4))
+
+        Hv = H.rearrange("b (p j) k -> b p j k", j=J)
+        O0v = out_0.rearrange("b (p j) f -> b p j f", j=J)
+        O1v = out_1.rearrange("b (p j) f -> b p (j f)", j=J)
+
+        hraw = {}
+
+        def load(q):
+            b, c = divmod(q, NCH)
+            t = hpool.tile([P, CH, K], BF16, name="hraw", tag="hraw")
+            nc.sync.dma_start(out=t[:], in_=Hv[b, :, c * CH : (c + 1) * CH, :])
+            hraw[q] = t
+
+        gb = const.tile([P, P], BF16, name="gb")
+        nc.vector.memset(gb[:], 0.0)
+        nc.scalar.dma_start(out=gb[0:4, :], in_=gamma.rearrange("(t p) -> t p", p=P))
+        nc.scalar.dma_start(out=gb[4:8, :], in_=beta.rearrange("(t p) -> t p", p=P))
+        load(0)
+        wraw = const.tile([P, 4, FEAT], BF16, name="wraw")
+        nc.sync.dma_start(out=wraw[:], in_=W.rearrange("(p t) f -> p t f", t=4))
+        for q in range(1, LOOK):
+            load(q)
+
+        identF = const.tile([P, P], F32, name="identF")
+        masks.make_identity(nc, identF[:])
+        identB = const.tile([P, P], BF16, name="identB")
+        masks.make_identity(nc, identB[:])
+
+        wg = const.tile([P, FEAT * 4], BF16, name="wg", align_bytes=64)
+        nc.vector.tensor_copy(
+            out=wg[:].rearrange("p (f t) -> p f t", t=4), in_=wraw[:].rearrange("p t f -> p f t")
+        )
+        wc = const.tile([P, FEAT], U32, name="wc", align_bytes=64)
+        ws = const.tile([P, FEAT], U8, name="ws", align_bytes=64)
+        nc.vector.quantize_mx(out=wc[:].bitcast(FP8X4), scales=ws[:], in_=wg[:])
+
+        rt = const.tile([P, P], F32, name="rt")
+        nc.gpsimd.memset(rt[:], 0.0)
+        nc.gpsimd.memset(rt[0:32, 0:128:2], 1.0)
+        nc.gpsimd.memset(rt[32:64, 0:128:126], 1.0)
+        nc.gpsimd.memset(rt[64:96, 1:128:126], 1.0)
+
+        Z = []
+        for i in range(NZ):
+            zt = const.tile([P, FT, ZW], F32, name="z%d" % i)
+            nc.gpsimd.memset(zt[:].rearrange("p f (r c) -> p f r c", c=WIN)[:, :, :, 0:6], 0.0)
+            Z.append(zt)
+        zm0 = const.tile([P, FT, 136], F32, name="zm0")
+        nc.gpsimd.memset(zm0[:], 0.0)
+        zm31 = const.tile([P, FT, 136], F32, name="zm31")
+        nc.gpsimd.memset(zm31[:], 0.0)
+        neghalf = const.tile([P, FT], F32, name="neghalf")
+        nc.gpsimd.memset(neghalf[:], -0.5)
+
+        gbT = const.tile([P, 8], F32, name="gbT")
+        msk = const.tile([P, 8], F32, name="msk")
+        tab = const.tile([P, 8], F32, name="tab")
+        dA = tab[:, 0:1]
+        ratio0 = tab[:, 1:2]
+        ratio31 = tab[:, 2:3]
+        dcol0 = tab[:, 3:4]
+        dcol31 = tab[:, 4:5]
+
+        def small_tables():
+            gb_ps = psT.tile([P, P], BF16, name="gb_ps", tag="t")
+            nc.tensor.transpose(out=gb_ps[:], in_=gb[:], identity=identB[:])
+            nc.vector.tensor_copy(out=gbT[:], in_=gb_ps[:, 0:8])
+            tab_ps = psT.tile([P, P], F32, name="tab_ps", tag="t")
+            nc.tensor.transpose(out=tab_ps[:], in_=rt[:], identity=identF[:])
+            nc.vector.tensor_copy(out=msk[:, 0:3], in_=tab_ps[:, 0:96:32])
+            m_even = msk[:, 0:1]
+            m_c0 = msk[:, 1:2]
+            m_c1 = msk[:, 2:3]
+            nc.vector.tensor_add(out=msk[:, 3:4], in0=m_c0, in1=m_c1)
+            nc.vector.tensor_scalar(out=dA, in0=msk[:, 3:4], scalar1=D6 - D9, scalar2=D9, op0=ALU.mult, op1=ALU.add)
+            nc.vector.tensor_scalar(out=msk[:, 4:5], in0=m_even, scalar1=R69 - 1.0, scalar2=1.0, op0=ALU.mult, op1=ALU.add)
+            nc.vector.tensor_scalar(out=msk[:, 5:6], in0=m_even, scalar1=1.0 - R69, scalar2=R69, op0=ALU.mult, op1=ALU.add)
+            nc.vector.scalar_tensor_tensor(out=ratio0, in0=m_c0, scalar=R46 - R69, in1=msk[:, 4:5], op0=ALU.mult, op1=ALU.add)
+            nc.vector.scalar_tensor_tensor(out=ratio31, in0=m_c1, scalar=R46 - R69, in1=msk[:, 5:6], op0=ALU.mult, op1=ALU.add)
+            nc.vector.tensor_scalar_mul(out=tab[:, 3:5], in0=tab[:, 1:3], scalar1=dA)
+
+        stats = const.tile([P, FT, NQ, 6], F32, name="stats")
+        grouped = {}
+        hc = {}
+        hs = {}
+
+        def flip(q):
+            G = gpool.tile([P, CH * P * 4], BF16, name="G", tag="G", align_bytes=64)
+            Gw = G[:].bitcast(F32)
+            for h in range(2):
+                xt = psT.tile([P, 512], F32, name="xt", tag="t")
+                for jl in range(2):
+                    words = hraw[q][:, 2 * h + jl, :].bitcast(F32)
+                    for u in range(2):
+                        s = 2 * jl + u
+                        nc.tensor.transpose(
+                            out=xt[:, s * P : (s + 1) * P], in_=words[:, u:256:2], identity=identF[:]
+                        )
+                nc.scalar.copy(
+                    out=Gw[:, h * 512 : (h + 1) * 512].rearrange("p (j r u) -> p j r u", j=2, u=2),
+                    in_=xt[:].rearrange("p (j u r) -> p j r u", j=2, u=2),
+                )
+            grouped[q] = G
+
+        def quant(q):
+            c_t = const.tile([P, 512], U32, name="hc%d" % q, align_bytes=64)
+            s_t = const.tile([P, 512], U8, name="hs%d" % q, align_bytes=64)
+            nc.vector.quantize_mx(out=c_t[:].bitcast(FP8X4), scales=s_t[:], in_=grouped[q][:])
+            hc[q] = c_t
+            hs[q] = s_t
+
+        def mult(q, ft):
+            Y = psY.tile([P, 512], F32, name="Y", tag="y")
+            nc.tensor.matmul_mx(
+                out=Y[:],
+                lhsT=wc[:, ft * P : (ft + 1) * P].bitcast(FP8X4),
+                lhsT_scale=ws[:, ft * P : (ft + 1) * P],
+                rhs=hc[q][:].bitcast(FP8X4),
+                rhs_scale=hs[q][:],
+                start=True,
+                stop=True,
+            )
+            return Y
+
+        def mm_stats(q):
+            for ft in range(FT):
+                Y = mult(q, ft)
+                nc.vector.bn_stats(out=stats[:, ft, q, :], in_=Y[:])
+
+        for step in range(NQ + 2):
+            if step + LOOK < NQ:
+                load(step + LOOK)
+            if step < NQ:
+                flip(step)
+            if 1 <= step <= NQ:
+                quant(step - 1)
+            if step >= 2:
+                mm_stats(step - 2)
+            if step == 4:
+                small_tables()
+
+        mv = const.tile([P, FT, 2], F32, name="mv")
+        for ft in range(FT):
+            nc.vector.bn_aggr(out=mv[:, ft, :], in_=stats[:, ft, :, :].rearrange("p c s -> p (c s)"))
+        ve = const.tile([P, FT], F32, name="ve")
+        nc.vector.tensor_scalar_add(out=ve[:], in0=mv[:, :, 1], scalar1=EPS_BN)
+        rstd = const.tile([P, FT], F32, name="rstd")
+        nc.gpsimd.tensor_tensor(out=rstd[:], in0=ve[:], in1=neghalf[:], op=ALU.pow)
+        ab = const.tile([P, 2, FT], F32, name="ab")
+        nc.vector.tensor_mul(out=ab[:, 0, :], in0=gbT[:, 0:4], in1=rstd[:])
+        ma = const.tile([P, FT], F32, name="ma")
+        nc.vector.tensor_mul(out=ma[:], in0=mv[:, :, 0], in1=ab[:, 0, :])
+        nc.vector.tensor_sub(out=ab[:, 1, :], in0=gbT[:, 4:8], in1=ma[:])
+        ab9 = const.tile([P, 2, FT], F32, name="ab9")
+        nc.vector.tensor_scalar_mul(out=ab9[:], in0=ab[:], scalar1=D9)
+
+        def scale_cols(view, factor):
+            nc.gpsimd.tensor_scalar(
+                out=view, in0=view, scalar1=factor, scalar2=0.0, op0=ALU.mult, op1=ALU.add
+            )
+
+        def make_z(g):
+            c = g % NCH
+            zt = Z[g % NZ]
+            for ft in range(FT):
+                Y = mult(g, ft)
+                nc.scalar.activation(
+                    out=zt[:, ft, Z0 : Z0 + CH * WIN].rearrange("p (w c) -> p w c", c=WIN)[:, :, 0:P],
+                    in_=Y[:].rearrange("p (w c) -> p w c", c=P),
+                    func=ACT.Relu,
+                    bias=ab9[:, 1, ft : ft + 1],
+                    scale=ab9[:, 0, ft : ft + 1],
+                )
+            scale_cols(zt[:].rearrange("p f (r c) -> p f r c", c=WIN)[:, :, :, 0:6], R69)
+            if c == 0:
+                scale_cols(zt[:, :, Z0 : Z0 + P : 2], R69)
+                scale_cols(zt[:, :, Z0 : Z0 + P : 126], RC)
+                nc.gpsimd.tensor_copy(out=zm0[:, :, Z0 : Z0 + P : 2], in_=zt[:, :, Z0 + 1 : Z0 + P : 2])
+            if c == NCH - 1:
+                w3 = Z0 + 3 * WIN
+                scale_cols(zt[:, :, w3 + 1 : w3 + P : 2], R69)
+                scale_cols(zt[:, :, w3 + 1 : w3 + P : 126], RC)
+                nc.gpsimd.tensor_copy(out=zm31[:, :, Z0 + 1 : Z0 + P : 2], in_=zt[:, :, w3 : w3 + P : 2])
+
+        def sum_rows(src, base):
+            T = psT.tile([P, 512], F32, name="T", tag="t")
+            for ft in range(FT):
+                for w in range(3):
+                    o = base + 2 * (w - 1)
+                    nc.tensor.matmul(
+                        out=T[:, ft * P : (ft + 1) * P],
+                        lhsT=src[:, ft, o : o + P],
+                        rhs=identF[:],
+                        is_transpose=True,
+                        start=(w == 0),
+                        stop=(w == 2),
+                    )
+            return T
+
+        Ot = {}
+        F8t = {}
+
+        def slot(b, j):
+            c = j // CH
+            if (b, c) not in Ot:
+                Ot[(b, c)] = work.tile([P, CH, FEAT], F32, name="O", tag="O")
+            return Ot[(b, c)][:, j % CH, :]
+
+        def cast_vec(dst, src, n):
+            t530 = work.tile([P, n], F32, name="t530", tag="t530", bufs=2)
+            nc.vector.tensor_scalar_mul(out=t530[:], in0=src, scalar1=Y_SCALE)
+            nc.vector.tensor_copy(out=dst, in_=t530[:], saturate=False)
+
+        def finish_chunk(b, c):
+            O = Ot[(b, c)]
+            lo = 1 if c == 0 else 0
+            nc.sync.dma_start(out=O0v[b, :, c * CH + lo : (c + 1) * CH, :], in_=O[:, lo:CH, :])
+            g8 = c // 2
+            if (b, g8) not in F8t:
+                F8t[(b, g8)] = work.tile([P, 2 * CH * FEAT], FP8, name="F8", tag="F8", bufs=2)
+            F8 = F8t[(b, g8)]
+            base = (c % 2) * CH * FEAT
+            hi = CH - VCAST
+            nc.scalar.activation(
+                out=F8[:, base + lo * FEAT : base + hi * FEAT],
+                in_=O[:, lo:hi, :].rearrange("p j f -> p (j f)"),
+                func=ACT.Copy,
+                scale=Y_SCALE,
+                saturate=False,
+            )
+            cast_vec(
+                F8[:, base + hi * FEAT : base + CH * FEAT],
+                O[:, hi:CH, :].rearrange("p j f -> p (j f)"),
+                VCAST * FEAT,
+            )
+            if c % 2 == 1:
+                l8 = FEAT if g8 == 0 else 0
+                w8 = 2 * CH * FEAT
+                nc.sync.dma_start(
+                    out=O1v[b, :, g8 * w8 + l8 : (g8 + 1) * w8], in_=F8[:, l8:w8].bitcast(U8)
+                )
+
+        make_z(0)
+        st = {}
+        for g in range(NQ):
+            b, c = divmod(g, NCH)
+            if g + 1 < NQ:
+                make_z(g + 1)
+            zt = Z[g % NZ]
+            for jj in range(CH):
+                j = c * CH + jj
+                T = sum_rows(zt, Z0 + jj * WIN)
+                if j % 2 == 0:
+                    st["Tev"] = T
+                    if j >= 2:
+                        nc.vector.scalar_tensor_tensor(
+                            out=slot(b, j - 1), in0=T[:], scalar=dA, in1=st["m"][:], op0=ALU.mult, op1=ALU.add
+                        )
+                        if (j - 1) % CH == CH - 1:
+                            finish_chunk(b, (j - 1) // CH)
+                else:
+                    S = work.tile([P, FEAT], F32, name="S", tag="S")
+                    nc.scalar.activation(out=S[:], in_=T[:], func=ACT.Copy, scale=dA)
+                    if j == 1:
+                        m = keep2.tile([P, FEAT], F32, name="m0", tag="m0")
+                        st["m0"] = m
+                    else:
+                        m = work.tile([P, FEAT], F32, name="m", tag="m")
+                    nc.vector.scalar_tensor_tensor(
+                        out=m[:], in0=st["Tev"][:], scalar=dA, in1=S[:], op0=ALU.mult, op1=ALU.add
+                    )
+                    if j >= 3:
+                        nc.vector.tensor_add(out=slot(b, j - 1), in0=st["S"][:], in1=m[:])
+                    st["S"] = S
+                    st["m"] = m
+            if c == 0:
+                Tm0 = sum_rows(zm0, Z0)
+                sm0 = keep2.tile([P, FEAT], F32, name="sm0", tag="sm0")
+                nc.scalar.activation(out=sm0[:], in_=Tm0[:], func=ACT.Copy, scale=dcol31)
+                st["sm0"] = sm0
+            if c == NCH - 1:
+                nc.vector.scalar_tensor_tensor(
+                    out=slot(b, J - 1), in0=st["m"][:], scalar=ratio31, in1=st["sm0"][:], op0=ALU.mult, op1=ALU.add
+                )
+                finish_chunk(b, c)
+                Tm31 = sum_rows(zm31, Z0)
+                sm31 = keep2.tile([P, FEAT], F32, name="sm31", tag="sm31")
+                nc.scalar.activation(out=sm31[:], in_=Tm31[:], func=ACT.Copy, scale=dcol0)
+                o0 = keep2.tile([P, FEAT], F32, name="o0", tag="o0")
+                nc.vector.scalar_tensor_tensor(
+                    out=o0[:], in0=st["m0"][:], scalar=ratio0, in1=sm31[:], op0=ALU.mult, op1=ALU.add
+                )
+                nc.sync.dma_start(out=O0v[b, :, 0, :], in_=o0[:])
+                f80 = keep2.tile([P, FEAT], FP8, name="f80", tag="f80")
+                nc.scalar.activation(out=f80[:], in_=o0[:], func=ACT.Copy, scale=Y_SCALE, saturate=False)
+                nc.sync.dma_start(out=O1v[b, :, 0:FEAT], in_=f80[:].bitcast(U8))

@@ -24,8 +24,13 @@ FT = FEAT // P
 WIN = 130
 ZW = 5 * WIN
 Z0 = 4
-NZ = 3
+NZ = 4
 LOOK = 6
+AHEAD = 2
+GADD = True
+PRE_NUM, PRE_DEN = 0, 4
+SC_FT = 3
+SC_Q = (1, 2, 3, 5, 6, 7, 9, 10, 11, 13, 14)
 
 EPS_BN = 1e-5
 EPS_DEG = 1e-5
@@ -36,7 +41,7 @@ R69 = D6 / D9
 R46 = D4 / D6
 RC = D4 * D9 / (D6 * D6)
 Y_SCALE = 530.0
-VCAST = 1
+VCAST = 0
 
 
 def tile_graphconvolutionbatch_kernel(tc, H, W, gamma, beta, out_0, out_1):
@@ -59,7 +64,11 @@ def tile_graphconvolutionbatch_kernel(tc, H, W, gamma, beta, out_0, out_1):
         def load(q):
             b, c = divmod(q, NCH)
             t = hpool.tile([P, CH, K], BF16, name="hraw", tag="hraw")
-            nc.sync.dma_start(out=t[:], in_=Hv[b, :, c * CH : (c + 1) * CH, :])
+            if q == 0:
+                for jj in range(CH):
+                    nc.sync.dma_start(out=t[:, jj, :], in_=Hv[b, :, jj, :])
+            else:
+                nc.sync.dma_start(out=t[:], in_=Hv[b, :, c * CH : (c + 1) * CH, :])
             hraw[q] = t
 
         gb = const.tile([P, P], BF16, name="gb")
@@ -130,7 +139,10 @@ def tile_graphconvolutionbatch_kernel(tc, H, W, gamma, beta, out_0, out_1):
             nc.vector.scalar_tensor_tensor(out=ratio31, in0=m_c1, scalar=R46 - R69, in1=msk[:, 5:6], op0=ALU.mult, op1=ALU.add)
             nc.vector.tensor_scalar_mul(out=tab[:, 3:5], in0=tab[:, 1:3], scalar1=dA)
 
-        stats = const.tile([P, FT, NQ, 6], F32, name="stats")
+        stats = const.tile([P, FT, NQ + 1, 6], F32, name="stats")
+        sums = const.tile([P, 2, NQ], F32, name="sums")
+        negc = const.tile([P, 1], F32, name="negc")
+        nslot = {}
         grouped = {}
         hc = {}
         hs = {}
@@ -176,7 +188,20 @@ def tile_graphconvolutionbatch_kernel(tc, H, W, gamma, beta, out_0, out_1):
         def mm_stats(q):
             for ft in range(FT):
                 Y = mult(q, ft)
-                nc.vector.bn_stats(out=stats[:, ft, q, :], in_=Y[:])
+                if ft == SC_FT and q in SC_Q:
+                    i = SC_Q.index(q)
+                    junk = work.tile([P, 512], F32, name="junk", tag="junk", bufs=2)
+                    nc.scalar.activation(out=junk[:], in_=Y[:], func=ACT.Identity, accum_out=sums[:, 0, i : i + 1])
+                    if i == 0:
+                        nc.vector.tensor_scalar_mul(out=negc[:], in0=sums[:, 0, 0:1], scalar1=-1.0 / 512.0)
+                    junk2 = work.tile([P, 512], F32, name="junk2", tag="junk", bufs=2)
+                    nc.scalar.activation(
+                        out=junk2[:], in_=Y[:], func=ACT.Square, bias=negc[:, 0:1], accum_out=sums[:, 1, i : i + 1]
+                    )
+                else:
+                    s = nslot.get(ft, 0)
+                    nslot[ft] = s + 1
+                    nc.vector.bn_stats(out=stats[:, ft, s, :], in_=Y[:])
 
         for step in range(NQ + 2):
             if step + LOOK < NQ:
@@ -191,8 +216,21 @@ def tile_graphconvolutionbatch_kernel(tc, H, W, gamma, beta, out_0, out_1):
                 small_tables()
 
         mv = const.tile([P, FT, 2], F32, name="mv")
+        n_sc = 512.0 * len(SC_Q)
+        tot = const.tile([P, 2], F32, name="tot")
+        nc.vector.tensor_reduce(out=tot[:], in_=sums[:, :, 0 : len(SC_Q)], axis=mybir.AxisListType.X, op=ALU.add)
+        ent = stats[:, SC_FT, nslot[SC_FT], 0:3]
+        nc.vector.memset(ent[:, 0:1], n_sc)
+        nc.vector.tensor_scalar_mul(out=ent[:, 1:2], in0=tot[:, 0:1], scalar1=1.0 / n_sc)
+        dm = const.tile([P, 2], F32, name="dm")
+        nc.vector.tensor_add(out=dm[:, 0:1], in0=ent[:, 1:2], in1=negc[:])
+        nc.vector.tensor_mul(out=dm[:, 1:2], in0=dm[:, 0:1], in1=dm[:, 0:1])
+        nc.vector.scalar_tensor_tensor(
+            out=ent[:, 2:3], in0=dm[:, 1:2], scalar=-n_sc, in1=tot[:, 1:2], op0=ALU.mult, op1=ALU.add
+        )
         for ft in range(FT):
-            nc.vector.bn_aggr(out=mv[:, ft, :], in_=stats[:, ft, :, :].rearrange("p c s -> p (c s)"))
+            n_el = 6 * nslot[ft] + (3 if ft == SC_FT else 0)
+            nc.vector.bn_aggr(out=mv[:, ft, :], in_=stats[:, ft, :, :].rearrange("p c s -> p (c s)")[:, 0:n_el])
         ve = const.tile([P, FT], F32, name="ve")
         nc.vector.tensor_scalar_add(out=ve[:], in0=mv[:, :, 1], scalar1=EPS_BN)
         rstd = const.tile([P, FT], F32, name="rstd")
@@ -233,23 +271,39 @@ def tile_graphconvolutionbatch_kernel(tc, H, W, gamma, beta, out_0, out_1):
                 scale_cols(zt[:, :, w3 + 1 : w3 + P : 126], RC)
                 nc.gpsimd.tensor_copy(out=zm31[:, :, Z0 + 1 : Z0 + P : 2], in_=zt[:, :, w3 : w3 + P : 2])
 
-        def sum_rows(src, base):
+        def sum_rows(src, base, pre=None):
             T = psT.tile([P, 512], F32, name="T", tag="t")
             for ft in range(FT):
-                for w in range(3):
-                    o = base + 2 * (w - 1)
+                if pre is None:
+                    wins = [src[:, ft, base + 2 * (w - 1) : base + 2 * (w - 1) + P] for w in range(3)]
+                else:
+                    wins = [src[:, ft, base : base + P], pre[:, ft, :]]
+                for w in range(len(wins)):
                     nc.tensor.matmul(
                         out=T[:, ft * P : (ft + 1) * P],
-                        lhsT=src[:, ft, o : o + P],
+                        lhsT=wins[w],
                         rhs=identF[:],
                         is_transpose=True,
                         start=(w == 0),
-                        stop=(w == 2),
+                        stop=(w == len(wins) - 1),
                     )
             return T
 
+        pres = {}
+
+        def pre_add(g):
+            zt = Z[g % NZ]
+            for jj in range(PRE_NUM):
+                base = Z0 + jj * WIN
+                s2 = work.tile([P, FT, P], F32, name="s2", tag="s2", bufs=2 * max(PRE_NUM, 1) + 1)
+                nc.gpsimd.tensor_tensor(
+                    out=s2[:], in0=zt[:, :, base - 2 : base - 2 + P], in1=zt[:, :, base + 2 : base + 2 + P], op=ALU.add
+                )
+                pres[(g, jj)] = s2
+
         Ot = {}
         F8t = {}
+        st = {}
 
         def slot(b, j):
             c = j // CH
@@ -262,45 +316,68 @@ def tile_graphconvolutionbatch_kernel(tc, H, W, gamma, beta, out_0, out_1):
             nc.vector.tensor_scalar_mul(out=t530[:], in0=src, scalar1=Y_SCALE)
             nc.vector.tensor_copy(out=dst, in_=t530[:], saturate=False)
 
-        def finish_chunk(b, c):
+        def finish(b, c, a, e, first1, last1):
             O = Ot[(b, c)]
-            lo = 1 if c == 0 else 0
-            nc.sync.dma_start(out=O0v[b, :, c * CH + lo : (c + 1) * CH, :], in_=O[:, lo:CH, :])
+            nc.sync.dma_start(out=O0v[b, :, c * CH + a : c * CH + e, :], in_=O[:, a:e, :])
             g8 = c // 2
             if (b, g8) not in F8t:
                 F8t[(b, g8)] = work.tile([P, 2 * CH * FEAT], FP8, name="F8", tag="F8", bufs=2)
             F8 = F8t[(b, g8)]
             base = (c % 2) * CH * FEAT
-            hi = CH - VCAST
-            nc.scalar.activation(
-                out=F8[:, base + lo * FEAT : base + hi * FEAT],
-                in_=O[:, lo:hi, :].rearrange("p j f -> p (j f)"),
-                func=ACT.Copy,
-                scale=Y_SCALE,
-                saturate=False,
-            )
-            cast_vec(
-                F8[:, base + hi * FEAT : base + CH * FEAT],
-                O[:, hi:CH, :].rearrange("p j f -> p (j f)"),
-                VCAST * FEAT,
-            )
-            if c % 2 == 1:
-                l8 = FEAT if g8 == 0 else 0
+            for a2 in range(a, e, 2):
+                e2 = min(a2 + 2, e)
+                nc.scalar.activation(
+                    out=F8[:, base + a2 * FEAT : base + e2 * FEAT],
+                    in_=O[:, a2:e2, :].rearrange("p j f -> p (j f)"),
+                    func=ACT.Copy,
+                    scale=Y_SCALE,
+                    saturate=False,
+                )
+            if last1 > first1:
                 w8 = 2 * CH * FEAT
                 nc.sync.dma_start(
-                    out=O1v[b, :, g8 * w8 + l8 : (g8 + 1) * w8], in_=F8[:, l8:w8].bitcast(U8)
+                    out=O1v[b, :, g8 * w8 + first1 : g8 * w8 + last1], in_=F8[:, first1:last1].bitcast(U8)
                 )
 
-        make_z(0)
-        st = {}
+        def finish_chunk(b, c):
+            lo = 1 if c == 0 else 0
+            w4 = CH * FEAT
+            if b == BATCH - 1 and c == NCH - 2:
+                finish(b, c, lo, CH, 0, w4)
+            elif c % 2 == 1:
+                finish(b, c, lo, CH, FEAT if c == 1 else 0, 2 * w4)
+            else:
+                finish(b, c, lo, CH, 0, 0)
+
+        def seam_first_column(b):
+            Tm31 = sum_rows(zm31, Z0)
+            sm31 = keep2.tile([P, FEAT], F32, name="sm31", tag="sm31")
+            nc.scalar.activation(out=sm31[:], in_=Tm31[:], func=ACT.Copy, scale=dcol0)
+            o0 = keep2.tile([P, FEAT], F32, name="o0", tag="o0")
+            nc.vector.scalar_tensor_tensor(
+                out=o0[:], in0=st["m0"][:], scalar=ratio0, in1=sm31[:], op0=ALU.mult, op1=ALU.add
+            )
+            nc.sync.dma_start(out=O0v[b, :, 0, :], in_=o0[:])
+            f80 = keep2.tile([P, FEAT], FP8, name="f80", tag="f80")
+            nc.scalar.activation(out=f80[:], in_=o0[:], func=ACT.Copy, scale=Y_SCALE, saturate=False)
+            nc.sync.dma_start(out=O1v[b, :, 0:FEAT], in_=f80[:].bitcast(U8))
+
+        for g in range(AHEAD):
+            make_z(g)
+            pre_add(g)
         for g in range(NQ):
             b, c = divmod(g, NCH)
-            if g + 1 < NQ:
-                make_z(g + 1)
+            if g + AHEAD < NQ:
+                make_z(g + AHEAD)
+                pre_add(g + AHEAD)
             zt = Z[g % NZ]
+            last = g == NQ - 1
+            w4 = CH * FEAT
+            if c == NCH - 1:
+                seam_first_column(b)
             for jj in range(CH):
                 j = c * CH + jj
-                T = sum_rows(zt, Z0 + jj * WIN)
+                T = sum_rows(zt, Z0 + jj * WIN, pres.get((g, jj)))
                 if j % 2 == 0:
                     st["Tev"] = T
                     if j >= 2:
@@ -309,9 +386,11 @@ def tile_graphconvolutionbatch_kernel(tc, H, W, gamma, beta, out_0, out_1):
                         )
                         if (j - 1) % CH == CH - 1:
                             finish_chunk(b, (j - 1) // CH)
+                        if last and jj == 2:
+                            finish(b, c, 0, 2, w4, w4 + 2 * FEAT)
                 else:
                     S = work.tile([P, FEAT], F32, name="S", tag="S")
-                    nc.scalar.activation(out=S[:], in_=T[:], func=ACT.Copy, scale=dA)
+                    nc.vector.tensor_scalar_mul(out=S[:], in0=T[:], scalar1=dA)
                     if j == 1:
                         m = keep2.tile([P, FEAT], F32, name="m0", tag="m0")
                         st["m0"] = m
@@ -321,7 +400,10 @@ def tile_graphconvolutionbatch_kernel(tc, H, W, gamma, beta, out_0, out_1):
                         out=m[:], in0=st["Tev"][:], scalar=dA, in1=S[:], op0=ALU.mult, op1=ALU.add
                     )
                     if j >= 3:
-                        nc.vector.tensor_add(out=slot(b, j - 1), in0=st["S"][:], in1=m[:])
+                        if GADD and not (last and jj == 3):
+                            nc.gpsimd.tensor_tensor(out=slot(b, j - 1), in0=st["S"][:], in1=m[:], op=ALU.add)
+                        else:
+                            nc.vector.tensor_add(out=slot(b, j - 1), in0=st["S"][:], in1=m[:])
                     st["S"] = S
                     st["m"] = m
             if c == 0:
@@ -330,18 +412,12 @@ def tile_graphconvolutionbatch_kernel(tc, H, W, gamma, beta, out_0, out_1):
                 nc.scalar.activation(out=sm0[:], in_=Tm0[:], func=ACT.Copy, scale=dcol31)
                 st["sm0"] = sm0
             if c == NCH - 1:
+                if last:
+                    finish(b, c, 2, 3, w4 + 2 * FEAT, w4 + 3 * FEAT)
                 nc.vector.scalar_tensor_tensor(
                     out=slot(b, J - 1), in0=st["m"][:], scalar=ratio31, in1=st["sm0"][:], op0=ALU.mult, op1=ALU.add
                 )
-                finish_chunk(b, c)
-                Tm31 = sum_rows(zm31, Z0)
-                sm31 = keep2.tile([P, FEAT], F32, name="sm31", tag="sm31")
-                nc.scalar.activation(out=sm31[:], in_=Tm31[:], func=ACT.Copy, scale=dcol0)
-                o0 = keep2.tile([P, FEAT], F32, name="o0", tag="o0")
-                nc.vector.scalar_tensor_tensor(
-                    out=o0[:], in0=st["m0"][:], scalar=ratio0, in1=sm31[:], op0=ALU.mult, op1=ALU.add
-                )
-                nc.sync.dma_start(out=O0v[b, :, 0, :], in_=o0[:])
-                f80 = keep2.tile([P, FEAT], FP8, name="f80", tag="f80")
-                nc.scalar.activation(out=f80[:], in_=o0[:], func=ACT.Copy, scale=Y_SCALE, saturate=False)
-                nc.sync.dma_start(out=O1v[b, :, 0:FEAT], in_=f80[:].bitcast(U8))
+                if last:
+                    finish(b, c, 3, 4, w4 + 3 * FEAT, 2 * w4)
+                else:
+                    finish_chunk(b, c)

@@ -139,6 +139,8 @@ def tile_graphconvolutionbatch_kernel(tc, H, W, gamma, beta, out_0, out_1):
             nc.vector.scalar_tensor_tensor(out=ratio31, in0=m_c1, scalar=R46 - R69, in1=msk[:, 5:6], op0=ALU.mult, op1=ALU.add)
             nc.vector.tensor_scalar_mul(out=tab[:, 3:5], in0=tab[:, 1:3], scalar1=dA)
 
+        ctx.enter_context(tc.manual_schedule(engines={mybir.EngineType.PE}))
+
         stats = const.tile([P, FT, NQ + 1, 6], F32, name="stats")
         sums = const.tile([P, 2, NQ], F32, name="sums")
         negc = const.tile([P, 1], F32, name="negc")
@@ -248,10 +250,10 @@ def tile_graphconvolutionbatch_kernel(tc, H, W, gamma, beta, out_0, out_1):
                 out=view, in0=view, scalar1=factor, scalar2=0.0, op0=ALU.mult, op1=ALU.add
             )
 
-        def make_z(g):
+        def make_z(g, fts):
             c = g % NCH
             zt = Z[g % NZ]
-            for ft in range(FT):
+            for ft in fts:
                 Y = mult(g, ft)
                 nc.scalar.activation(
                     out=zt[:, ft, Z0 : Z0 + CH * WIN].rearrange("p (w c) -> p w c", c=WIN)[:, :, 0:P],
@@ -260,6 +262,8 @@ def tile_graphconvolutionbatch_kernel(tc, H, W, gamma, beta, out_0, out_1):
                     bias=ab9[:, 1, ft : ft + 1],
                     scale=ab9[:, 0, ft : ft + 1],
                 )
+            if fts[-1] != FT - 1:
+                return
             scale_cols(zt[:].rearrange("p f (r c) -> p f r c", c=WIN)[:, :, :, 0:6], R69)
             if c == 0:
                 scale_cols(zt[:, :, Z0 : Z0 + P : 2], R69)
@@ -363,13 +367,9 @@ def tile_graphconvolutionbatch_kernel(tc, H, W, gamma, beta, out_0, out_1):
             nc.sync.dma_start(out=O1v[b, :, 0:FEAT], in_=f80[:].bitcast(U8))
 
         for g in range(AHEAD):
-            make_z(g)
-            pre_add(g)
+            make_z(g, (0, 1, 2, 3))
         for g in range(NQ):
             b, c = divmod(g, NCH)
-            if g + AHEAD < NQ:
-                make_z(g + AHEAD)
-                pre_add(g + AHEAD)
             zt = Z[g % NZ]
             last = g == NQ - 1
             w4 = CH * FEAT
@@ -377,6 +377,8 @@ def tile_graphconvolutionbatch_kernel(tc, H, W, gamma, beta, out_0, out_1):
                 seam_first_column(b)
             for jj in range(CH):
                 j = c * CH + jj
+                if jj % 2 == 0 and g + AHEAD < NQ:
+                    make_z(g + AHEAD, (jj, jj + 1))
                 T = sum_rows(zt, Z0 + jj * WIN, pres.get((g, jj)))
                 if j % 2 == 0:
                     st["Tev"] = T

@@ -25,12 +25,14 @@ WIN = 130
 ZW = 5 * WIN
 Z0 = 4
 NZ = 4
-LOOK = 6
+LOOK = 5
 AHEAD = 2
 GADD = True
 PRE_NUM, PRE_DEN = 0, 4
 SC_FT = 3
-SC_Q = (1, 2, 3, 5, 6, 7, 9, 10, 11, 13, 14)
+SC_Q = (1, 2, 3, 5, 6, 7, 9, 10, 11, 13)
+NE = 14
+PRE_G = (3,)
 
 EPS_BN = 1e-5
 EPS_DEG = 1e-5
@@ -42,16 +44,13 @@ R46 = D4 / D6
 RC = D4 * D9 / (D6 * D6)
 Y_SCALE = 530.0
 VCAST = 0
+SMB = 6
 
 
 def tile_graphconvolutionbatch_kernel(tc, H, W, gamma, beta, out_0, out_1):
     nc = tc.nc
     with ExitStack() as ctx:
         const = ctx.enter_context(tc.tile_pool(name="const", bufs=1))
-        hpool = ctx.enter_context(tc.tile_pool(name="hpool", bufs=8))
-        gpool = ctx.enter_context(tc.tile_pool(name="gpool", bufs=3))
-        work = ctx.enter_context(tc.tile_pool(name="work", bufs=3))
-        keep2 = ctx.enter_context(tc.tile_pool(name="keep2", bufs=2))
         psY = ctx.enter_context(tc.psum_pool(name="psY", bufs=4))
         psT = ctx.enter_context(tc.psum_pool(name="psT", bufs=4))
 
@@ -59,221 +58,262 @@ def tile_graphconvolutionbatch_kernel(tc, H, W, gamma, beta, out_0, out_1):
         O0v = out_0.rearrange("b (p j) f -> b p j f", j=J)
         O1v = out_1.rearrange("b (p j) f -> b p (j f)", j=J)
 
-        hraw = {}
+        with ExitStack() as p1:
+            hpool = p1.enter_context(tc.tile_pool(name="hpool", bufs=7))
+            gpool = p1.enter_context(tc.tile_pool(name="gpool", bufs=3))
+            hraw = {}
 
-        def load(q):
-            b, c = divmod(q, NCH)
-            t = hpool.tile([P, CH, K], BF16, name="hraw", tag="hraw")
-            if q == 0:
-                for jj in range(CH):
-                    nc.sync.dma_start(out=t[:, jj, :], in_=Hv[b, :, jj, :])
-            else:
-                nc.sync.dma_start(out=t[:], in_=Hv[b, :, c * CH : (c + 1) * CH, :])
-            hraw[q] = t
-
-        gb = const.tile([P, P], BF16, name="gb")
-        nc.vector.memset(gb[:], 0.0)
-        nc.scalar.dma_start(out=gb[0:4, :], in_=gamma.rearrange("(t p) -> t p", p=P))
-        nc.scalar.dma_start(out=gb[4:8, :], in_=beta.rearrange("(t p) -> t p", p=P))
-        load(0)
-        wraw = const.tile([P, 4, FEAT], BF16, name="wraw")
-        nc.sync.dma_start(out=wraw[:], in_=W.rearrange("(p t) f -> p t f", t=4))
-        for q in range(1, LOOK):
-            load(q)
-
-        identF = const.tile([P, P], F32, name="identF")
-        masks.make_identity(nc, identF[:])
-        identB = const.tile([P, P], BF16, name="identB")
-        masks.make_identity(nc, identB[:])
-
-        wg = const.tile([P, FEAT * 4], BF16, name="wg", align_bytes=64)
-        nc.vector.tensor_copy(
-            out=wg[:].rearrange("p (f t) -> p f t", t=4), in_=wraw[:].rearrange("p t f -> p f t")
-        )
-        wc = const.tile([P, FEAT], U32, name="wc", align_bytes=64)
-        ws = const.tile([P, FEAT], U8, name="ws", align_bytes=64)
-        nc.vector.quantize_mx(out=wc[:].bitcast(FP8X4), scales=ws[:], in_=wg[:])
-
-        rt = const.tile([P, P], F32, name="rt")
-        nc.gpsimd.memset(rt[:], 0.0)
-        nc.gpsimd.memset(rt[0:32, 0:128:2], 1.0)
-        nc.gpsimd.memset(rt[32:64, 0:128:126], 1.0)
-        nc.gpsimd.memset(rt[64:96, 1:128:126], 1.0)
-
-        Z = []
-        for i in range(NZ):
-            zt = const.tile([P, FT, ZW], F32, name="z%d" % i)
-            nc.gpsimd.memset(zt[:].rearrange("p f (r c) -> p f r c", c=WIN)[:, :, :, 0:6], 0.0)
-            Z.append(zt)
-        zm0 = const.tile([P, FT, 136], F32, name="zm0")
-        nc.gpsimd.memset(zm0[:], 0.0)
-        zm31 = const.tile([P, FT, 136], F32, name="zm31")
-        nc.gpsimd.memset(zm31[:], 0.0)
-        neghalf = const.tile([P, FT], F32, name="neghalf")
-        nc.gpsimd.memset(neghalf[:], -0.5)
-
-        gbT = const.tile([P, 8], F32, name="gbT")
-        msk = const.tile([P, 8], F32, name="msk")
-        tab = const.tile([P, 8], F32, name="tab")
-        dA = tab[:, 0:1]
-        ratio0 = tab[:, 1:2]
-        ratio31 = tab[:, 2:3]
-        dcol0 = tab[:, 3:4]
-        dcol31 = tab[:, 4:5]
-
-        def small_tables():
-            gb_ps = psT.tile([P, P], BF16, name="gb_ps", tag="t")
-            nc.tensor.transpose(out=gb_ps[:], in_=gb[:], identity=identB[:])
-            nc.vector.tensor_copy(out=gbT[:], in_=gb_ps[:, 0:8])
-            tab_ps = psT.tile([P, P], F32, name="tab_ps", tag="t")
-            nc.tensor.transpose(out=tab_ps[:], in_=rt[:], identity=identF[:])
-            nc.vector.tensor_copy(out=msk[:, 0:3], in_=tab_ps[:, 0:96:32])
-            m_even = msk[:, 0:1]
-            m_c0 = msk[:, 1:2]
-            m_c1 = msk[:, 2:3]
-            nc.vector.tensor_add(out=msk[:, 3:4], in0=m_c0, in1=m_c1)
-            nc.vector.tensor_scalar(out=dA, in0=msk[:, 3:4], scalar1=D6 - D9, scalar2=D9, op0=ALU.mult, op1=ALU.add)
-            nc.vector.tensor_scalar(out=msk[:, 4:5], in0=m_even, scalar1=R69 - 1.0, scalar2=1.0, op0=ALU.mult, op1=ALU.add)
-            nc.vector.tensor_scalar(out=msk[:, 5:6], in0=m_even, scalar1=1.0 - R69, scalar2=R69, op0=ALU.mult, op1=ALU.add)
-            nc.vector.scalar_tensor_tensor(out=ratio0, in0=m_c0, scalar=R46 - R69, in1=msk[:, 4:5], op0=ALU.mult, op1=ALU.add)
-            nc.vector.scalar_tensor_tensor(out=ratio31, in0=m_c1, scalar=R46 - R69, in1=msk[:, 5:6], op0=ALU.mult, op1=ALU.add)
-            nc.vector.tensor_scalar_mul(out=tab[:, 3:5], in0=tab[:, 1:3], scalar1=dA)
-
-        ctx.enter_context(tc.manual_schedule(engines={mybir.EngineType.PE}))
-
-        stats = const.tile([P, FT, NQ + 1, 6], F32, name="stats")
-        sums = const.tile([P, 2, NQ], F32, name="sums")
-        negc = const.tile([P, 1], F32, name="negc")
-        nslot = {}
-        grouped = {}
-        hc = {}
-        hs = {}
-
-        def flip(q):
-            G = gpool.tile([P, CH * P * 4], BF16, name="G", tag="G", align_bytes=64)
-            Gw = G[:].bitcast(F32)
-            for h in range(2):
-                xt = psT.tile([P, 512], F32, name="xt", tag="t")
-                for jl in range(2):
-                    words = hraw[q][:, 2 * h + jl, :].bitcast(F32)
-                    for u in range(2):
-                        s = 2 * jl + u
-                        nc.tensor.transpose(
-                            out=xt[:, s * P : (s + 1) * P], in_=words[:, u:256:2], identity=identF[:]
-                        )
-                nc.scalar.copy(
-                    out=Gw[:, h * 512 : (h + 1) * 512].rearrange("p (j r u) -> p j r u", j=2, u=2),
-                    in_=xt[:].rearrange("p (j u r) -> p j r u", j=2, u=2),
-                )
-            grouped[q] = G
-
-        def quant(q):
-            c_t = const.tile([P, 512], U32, name="hc%d" % q, align_bytes=64)
-            s_t = const.tile([P, 512], U8, name="hs%d" % q, align_bytes=64)
-            nc.vector.quantize_mx(out=c_t[:].bitcast(FP8X4), scales=s_t[:], in_=grouped[q][:])
-            hc[q] = c_t
-            hs[q] = s_t
-
-        def mult(q, ft):
-            Y = psY.tile([P, 512], F32, name="Y", tag="y")
-            nc.tensor.matmul_mx(
-                out=Y[:],
-                lhsT=wc[:, ft * P : (ft + 1) * P].bitcast(FP8X4),
-                lhsT_scale=ws[:, ft * P : (ft + 1) * P],
-                rhs=hc[q][:].bitcast(FP8X4),
-                rhs_scale=hs[q][:],
-                start=True,
-                stop=True,
-            )
-            return Y
-
-        def mm_stats(q):
-            for ft in range(FT):
-                Y = mult(q, ft)
-                if ft == SC_FT and q in SC_Q:
-                    i = SC_Q.index(q)
-                    junk = work.tile([P, 512], F32, name="junk", tag="junk", bufs=2)
-                    nc.scalar.activation(out=junk[:], in_=Y[:], func=ACT.Identity, accum_out=sums[:, 0, i : i + 1])
-                    if i == 0:
-                        nc.vector.tensor_scalar_mul(out=negc[:], in0=sums[:, 0, 0:1], scalar1=-1.0 / 512.0)
-                    junk2 = work.tile([P, 512], F32, name="junk2", tag="junk", bufs=2)
-                    nc.scalar.activation(
-                        out=junk2[:], in_=Y[:], func=ACT.Square, bias=negc[:, 0:1], accum_out=sums[:, 1, i : i + 1]
-                    )
+            def load(q):
+                b, c = divmod(q, NCH)
+                t = hpool.tile([P, CH, K], BF16, name="hraw", tag="hraw")
+                if q == 0:
+                    for jj in range(CH):
+                        nc.sync.dma_start(out=t[:, jj, :], in_=Hv[b, :, jj, :])
                 else:
-                    s = nslot.get(ft, 0)
-                    nslot[ft] = s + 1
-                    nc.vector.bn_stats(out=stats[:, ft, s, :], in_=Y[:])
+                    nc.sync.dma_start(out=t[:], in_=Hv[b, :, c * CH : (c + 1) * CH, :])
+                hraw[q] = t
 
-        for step in range(NQ + 2):
-            if step + LOOK < NQ:
-                load(step + LOOK)
-            if step < NQ:
-                flip(step)
-            if 1 <= step <= NQ:
-                quant(step - 1)
-            if step >= 2:
-                mm_stats(step - 2)
-            if step == 4:
-                small_tables()
+            gb = const.tile([P, P], BF16, name="gb")
+            nc.vector.memset(gb[:], 0.0)
+            nc.scalar.dma_start(out=gb[0:4, :], in_=gamma.rearrange("(t p) -> t p", p=P))
+            nc.scalar.dma_start(out=gb[4:8, :], in_=beta.rearrange("(t p) -> t p", p=P))
+            load(0)
+            wraw = const.tile([P, 4, FEAT], BF16, name="wraw")
+            nc.sync.dma_start(out=wraw[:], in_=W.rearrange("(p t) f -> p t f", t=4))
+            for q in range(1, LOOK):
+                load(q)
+
+            identF = const.tile([P, P], F32, name="identF")
+            masks.make_identity(nc, identF[:])
+            identB = const.tile([P, P], BF16, name="identB")
+            masks.make_identity(nc, identB[:])
+
+            wg = const.tile([P, FEAT * 4], BF16, name="wg", align_bytes=64)
+            nc.vector.tensor_copy(
+                out=wg[:].rearrange("p (f t) -> p f t", t=4), in_=wraw[:].rearrange("p t f -> p f t")
+            )
+            wc = const.tile([P, FEAT], U32, name="wc", align_bytes=64)
+            ws = const.tile([P, FEAT], U8, name="ws", align_bytes=64)
+            nc.vector.quantize_mx(out=wc[:].bitcast(FP8X4), scales=ws[:], in_=wg[:])
+
+            rt = const.tile([P, P], F32, name="rt")
+            nc.gpsimd.memset(rt[:], 0.0)
+            nc.gpsimd.memset(rt[0:32, 0:128:2], 1.0)
+            nc.gpsimd.memset(rt[32:64, 0:128:126], 1.0)
+            nc.gpsimd.memset(rt[64:96, 1:128:126], 1.0)
+
+            Z = []
+            for i in range(NZ):
+                zt = const.tile([P, FT, ZW], F32, name="z%d" % i)
+                nc.gpsimd.memset(zt[:].rearrange("p f (r c) -> p f r c", c=WIN)[:, :, :, 0:6], 0.0)
+                Z.append(zt)
+            zmix = []
+            for i in range(BATCH):
+                zx = const.tile([P, FT, 136], F32, name="zmix%d" % i)
+                nc.gpsimd.memset(zx[:], 0.0)
+                zmix.append(zx)
+            neghalf = const.tile([P, FT], F32, name="neghalf")
+            nc.gpsimd.memset(neghalf[:], -0.5)
+
+            gbT = const.tile([P, 8], F32, name="gbT")
+            gb9 = const.tile([P, 8], F32, name="gb9")
+            msk = const.tile([P, 8], F32, name="msk")
+            tab = const.tile([P, 8], F32, name="tab")
+            dA = tab[:, 0:1]
+            ratio0 = tab[:, 1:2]
+            ratio31 = tab[:, 2:3]
+            dcol0 = tab[:, 3:4]
+            dcol31 = tab[:, 4:5]
+
+            def small_tables():
+                gb_ps = psT.tile([P, P], BF16, name="gb_ps", tag="t")
+                nc.tensor.transpose(out=gb_ps[:], in_=gb[:], identity=identB[:])
+                nc.vector.tensor_copy(out=gbT[:], in_=gb_ps[:, 0:8])
+                nc.vector.tensor_scalar_mul(out=gb9[:], in0=gbT[:], scalar1=D9)
+                tab_ps = psT.tile([P, P], F32, name="tab_ps", tag="t")
+                nc.tensor.transpose(out=tab_ps[:], in_=rt[:], identity=identF[:])
+                nc.vector.tensor_copy(out=msk[:, 0:3], in_=tab_ps[:, 0:96:32])
+                m_even = msk[:, 0:1]
+                m_c0 = msk[:, 1:2]
+                m_c1 = msk[:, 2:3]
+                nc.vector.tensor_add(out=msk[:, 3:4], in0=m_c0, in1=m_c1)
+                nc.vector.tensor_scalar(out=dA, in0=msk[:, 3:4], scalar1=D6 - D9, scalar2=D9, op0=ALU.mult, op1=ALU.add)
+                nc.vector.tensor_scalar(out=msk[:, 4:5], in0=m_even, scalar1=R69 - 1.0, scalar2=1.0, op0=ALU.mult, op1=ALU.add)
+                nc.vector.tensor_scalar(out=msk[:, 5:6], in0=m_even, scalar1=1.0 - R69, scalar2=R69, op0=ALU.mult, op1=ALU.add)
+                nc.vector.scalar_tensor_tensor(out=ratio0, in0=m_c0, scalar=R46 - R69, in1=msk[:, 4:5], op0=ALU.mult, op1=ALU.add)
+                nc.vector.scalar_tensor_tensor(out=ratio31, in0=m_c1, scalar=R46 - R69, in1=msk[:, 5:6], op0=ALU.mult, op1=ALU.add)
+                nc.vector.tensor_scalar_mul(out=tab[:, 5:7], in0=tab[:, 1:3], scalar1=dA)
+                nc.vector.tensor_scalar(out=msk[:, 6:7], in0=m_even, scalar1=-1.0, scalar2=1.0, op0=ALU.mult, op1=ALU.add)
+                nc.vector.tensor_mul(out=dcol0, in0=tab[:, 5:6], in1=msk[:, 6:7])
+                nc.vector.tensor_mul(out=dcol31, in0=tab[:, 6:7], in1=m_even)
+
+            ctx.enter_context(tc.manual_schedule(engines={mybir.EngineType.PE}))
+
+            NL = NQ - NE
+            statsE = const.tile([P, FT, NE + 1, 6], F32, name="statsE")
+            statsL = const.tile([P, FT, 3 + 6 * NL], F32, name="statsL")
+            nc.vector.memset(statsL[:, :, 0:1], 512.0 * NE)
+            pm = const.tile([P, FT, 2], F32, name="pm")
+            tot = const.tile([P, 2], F32, name="tot")
+            dm = const.tile([P, 2], F32, name="dm")
+            sums = const.tile([P, 2, NQ], F32, name="sums")
+            negc = const.tile([P, 1], F32, name="negc")
+            nslot = {}
+            ycp = {}
+            grouped = {}
+            hc = {}
+            hs = {}
+
+            def flip(q):
+                G = gpool.tile([P, CH * P * 4], BF16, name="G", tag="G", align_bytes=64)
+                Gw = G[:].bitcast(F32)
+                for h in range(2):
+                    xt = psT.tile([P, 512], F32, name="xt", tag="t")
+                    for jl in range(2):
+                        words = hraw[q][:, 2 * h + jl, :].bitcast(F32)
+                        for u in range(2):
+                            s = 2 * jl + u
+                            nc.tensor.transpose(
+                                out=xt[:, s * P : (s + 1) * P], in_=words[:, u:256:2], identity=identF[:]
+                            )
+                    nc.scalar.copy(
+                        out=Gw[:, h * 512 : (h + 1) * 512].rearrange("p (j r u) -> p j r u", j=2, u=2),
+                        in_=xt[:].rearrange("p (j u r) -> p j r u", j=2, u=2),
+                    )
+                grouped[q] = G
+
+            def quant(q):
+                c_t = const.tile([P, 512], U32, name="hc%d" % q, align_bytes=64)
+                s_t = const.tile([P, 512], U8, name="hs%d" % q, align_bytes=64)
+                nc.vector.quantize_mx(out=c_t[:].bitcast(FP8X4), scales=s_t[:], in_=grouped[q][:])
+                hc[q] = c_t
+                hs[q] = s_t
+
+            def mult(q, ft):
+                Y = psY.tile([P, 512], F32, name="Y", tag="y")
+                nc.tensor.matmul_mx(
+                    out=Y[:],
+                    lhsT=wc[:, ft * P : (ft + 1) * P].bitcast(FP8X4),
+                    lhsT_scale=ws[:, ft * P : (ft + 1) * P],
+                    rhs=hc[q][:].bitcast(FP8X4),
+                    rhs_scale=hs[q][:],
+                    start=True,
+                    stop=True,
+                )
+                return Y
+
+            def mm_stats(q):
+                for ft in range(FT):
+                    Y = mult(q, ft)
+                    if ft == SC_FT and q in SC_Q:
+                        i = SC_Q.index(q)
+                        yc = const.tile([P, 512], F32, name="ycp%d" % q)
+                        ycp[q] = yc
+                        nc.scalar.activation(out=yc[:], in_=Y[:], func=ACT.Identity, accum_out=sums[:, 0, i : i + 1])
+                        if i == 0:
+                            nc.vector.tensor_scalar_mul(out=negc[:], in0=sums[:, 0, 0:1], scalar1=-1.0 / 512.0)
+                        junk2 = gpool.tile([P, 512], F32, name="junk2", tag="junk", bufs=2)
+                        nc.scalar.activation(
+                            out=junk2[:], in_=Y[:], func=ACT.Square, bias=negc[:, 0:1], accum_out=sums[:, 1, i : i + 1]
+                        )
+                    elif q < NE:
+                        s = nslot.get(ft, 0)
+                        nslot[ft] = s + 1
+                        nc.vector.bn_stats(out=statsE[:, ft, s, :], in_=Y[:])
+                    else:
+                        o = 3 + 6 * (q - NE)
+                        nc.vector.bn_stats(out=statsL[:, ft, o : o + 6], in_=Y[:])
+
+            def early_aggr():
+                n_sc = 512.0 * len(SC_Q)
+                nc.vector.tensor_reduce(out=tot[:], in_=sums[:, :, 0 : len(SC_Q)], axis=mybir.AxisListType.X, op=ALU.add)
+                ent = statsE[:, SC_FT, nslot[SC_FT], 0:3]
+                nc.vector.memset(ent[:, 0:1], n_sc)
+                nc.vector.tensor_scalar_mul(out=ent[:, 1:2], in0=tot[:, 0:1], scalar1=1.0 / n_sc)
+                nc.vector.tensor_add(out=dm[:, 0:1], in0=ent[:, 1:2], in1=negc[:])
+                nc.vector.tensor_mul(out=dm[:, 1:2], in0=dm[:, 0:1], in1=dm[:, 0:1])
+                nc.vector.scalar_tensor_tensor(
+                    out=ent[:, 2:3], in0=dm[:, 1:2], scalar=-n_sc, in1=tot[:, 1:2], op0=ALU.mult, op1=ALU.add
+                )
+                for ft in range(FT):
+                    n_el = 6 * nslot[ft] + (3 if ft == SC_FT else 0)
+                    nc.vector.bn_aggr(out=pm[:, ft, :], in_=statsE[:, ft, :, :].rearrange("p c s -> p (c s)")[:, 0:n_el])
+                nc.vector.tensor_copy(out=statsL[:, :, 1:2], in_=pm[:, :, 0:1])
+                nc.vector.tensor_scalar_mul(out=statsL[:, :, 2:3], in0=pm[:, :, 1:2], scalar1=512.0 * NE)
+
+            for step in range(NQ + 2):
+                if step + LOOK < NQ:
+                    load(step + LOOK)
+                if step < NQ:
+                    flip(step)
+                if 1 <= step <= NQ:
+                    quant(step - 1)
+                if step >= 2:
+                    mm_stats(step - 2)
+                if step == 4:
+                    small_tables()
+                if step == NE + 1:
+                    early_aggr()
 
         mv = const.tile([P, FT, 2], F32, name="mv")
-        n_sc = 512.0 * len(SC_Q)
-        tot = const.tile([P, 2], F32, name="tot")
-        nc.vector.tensor_reduce(out=tot[:], in_=sums[:, :, 0 : len(SC_Q)], axis=mybir.AxisListType.X, op=ALU.add)
-        ent = stats[:, SC_FT, nslot[SC_FT], 0:3]
-        nc.vector.memset(ent[:, 0:1], n_sc)
-        nc.vector.tensor_scalar_mul(out=ent[:, 1:2], in0=tot[:, 0:1], scalar1=1.0 / n_sc)
-        dm = const.tile([P, 2], F32, name="dm")
-        nc.vector.tensor_add(out=dm[:, 0:1], in0=ent[:, 1:2], in1=negc[:])
-        nc.vector.tensor_mul(out=dm[:, 1:2], in0=dm[:, 0:1], in1=dm[:, 0:1])
-        nc.vector.scalar_tensor_tensor(
-            out=ent[:, 2:3], in0=dm[:, 1:2], scalar=-n_sc, in1=tot[:, 1:2], op0=ALU.mult, op1=ALU.add
-        )
         for ft in range(FT):
-            n_el = 6 * nslot[ft] + (3 if ft == SC_FT else 0)
-            nc.vector.bn_aggr(out=mv[:, ft, :], in_=stats[:, ft, :, :].rearrange("p c s -> p (c s)")[:, 0:n_el])
+            nc.vector.bn_aggr(out=mv[:, ft, :], in_=statsL[:, ft, :])
         ve = const.tile([P, FT], F32, name="ve")
         nc.vector.tensor_scalar_add(out=ve[:], in0=mv[:, :, 1], scalar1=EPS_BN)
         rstd = const.tile([P, FT], F32, name="rstd")
         nc.gpsimd.tensor_tensor(out=rstd[:], in0=ve[:], in1=neghalf[:], op=ALU.pow)
-        ab = const.tile([P, 2, FT], F32, name="ab")
-        nc.vector.tensor_mul(out=ab[:, 0, :], in0=gbT[:, 0:4], in1=rstd[:])
-        ma = const.tile([P, FT], F32, name="ma")
-        nc.vector.tensor_mul(out=ma[:], in0=mv[:, :, 0], in1=ab[:, 0, :])
-        nc.vector.tensor_sub(out=ab[:, 1, :], in0=gbT[:, 4:8], in1=ma[:])
         ab9 = const.tile([P, 2, FT], F32, name="ab9")
-        nc.vector.tensor_scalar_mul(out=ab9[:], in0=ab[:], scalar1=D9)
+        nc.vector.tensor_mul(out=ab9[:, 0, :], in0=gb9[:, 0:4], in1=rstd[:])
+        ma = const.tile([P, FT], F32, name="ma")
+        nc.vector.tensor_mul(out=ma[:], in0=mv[:, :, 0], in1=ab9[:, 0, :])
+        nc.vector.tensor_sub(out=ab9[:, 1, :], in0=gb9[:, 4:8], in1=ma[:])
 
+        work = ctx.enter_context(tc.tile_pool(name="work", bufs=3))
+        keep2 = ctx.enter_context(tc.tile_pool(name="keep2", bufs=2))
         def scale_cols(view, factor):
             nc.gpsimd.tensor_scalar(
                 out=view, in0=view, scalar1=factor, scalar2=0.0, op0=ALU.mult, op1=ALU.add
             )
 
-        def make_z(g, fts):
+        def make_z(g, fts, vec_fts=()):
             c = g % NCH
             zt = Z[g % NZ]
             for ft in fts:
-                Y = mult(g, ft)
-                nc.scalar.activation(
-                    out=zt[:, ft, Z0 : Z0 + CH * WIN].rearrange("p (w c) -> p w c", c=WIN)[:, :, 0:P],
-                    in_=Y[:].rearrange("p (w c) -> p w c", c=P),
-                    func=ACT.Relu,
-                    bias=ab9[:, 1, ft : ft + 1],
-                    scale=ab9[:, 0, ft : ft + 1],
-                )
-            if fts[-1] != FT - 1:
-                return
+                Y = ycp[g] if ft == SC_FT and g in SC_Q else mult(g, ft)
+                z_out = zt[:, ft, Z0 : Z0 + CH * WIN].rearrange("p (w c) -> p w c", c=WIN)[:, :, 0:P]
+                y_in = Y[:].rearrange("p (w c) -> p w c", c=P)
+                if ft in vec_fts:
+                    nc.vector.tensor_scalar(
+                        out=z_out,
+                        in0=y_in,
+                        scalar1=ab9[:, 0, ft : ft + 1],
+                        scalar2=ab9[:, 1, ft : ft + 1],
+                        op0=ALU.mult,
+                        op1=ALU.add,
+                    )
+                    nc.vector.tensor_scalar_max(out=z_out, in0=z_out, scalar1=0.0)
+                else:
+                    nc.scalar.activation(
+                        out=z_out,
+                        in_=y_in,
+                        func=ACT.Relu,
+                        bias=ab9[:, 1, ft : ft + 1],
+                        scale=ab9[:, 0, ft : ft + 1],
+                    )
+
+        def edges(g):
+            c = g % NCH
+            zt = Z[g % NZ]
             scale_cols(zt[:].rearrange("p f (r c) -> p f r c", c=WIN)[:, :, :, 0:6], R69)
             if c == 0:
                 scale_cols(zt[:, :, Z0 : Z0 + P : 2], R69)
                 scale_cols(zt[:, :, Z0 : Z0 + P : 126], RC)
-                nc.gpsimd.tensor_copy(out=zm0[:, :, Z0 : Z0 + P : 2], in_=zt[:, :, Z0 + 1 : Z0 + P : 2])
+                nc.gpsimd.tensor_copy(out=zmix[g // NCH][:, :, Z0 : Z0 + P : 2], in_=zt[:, :, Z0 + 1 : Z0 + P : 2])
             if c == NCH - 1:
                 w3 = Z0 + 3 * WIN
                 scale_cols(zt[:, :, w3 + 1 : w3 + P : 2], R69)
                 scale_cols(zt[:, :, w3 + 1 : w3 + P : 126], RC)
-                nc.gpsimd.tensor_copy(out=zm31[:, :, Z0 + 1 : Z0 + P : 2], in_=zt[:, :, w3 : w3 + P : 2])
+                nc.gpsimd.tensor_copy(out=zmix[g // NCH][:, :, Z0 + 1 : Z0 + P : 2], in_=zt[:, :, w3 : w3 + P : 2])
 
         def sum_rows(src, base, pre=None):
             T = psT.tile([P, 512], F32, name="T", tag="t")
@@ -297,9 +337,9 @@ def tile_graphconvolutionbatch_kernel(tc, H, W, gamma, beta, out_0, out_1):
 
         def pre_add(g):
             zt = Z[g % NZ]
-            for jj in range(PRE_NUM):
+            for jj in PRE_G:
                 base = Z0 + jj * WIN
-                s2 = work.tile([P, FT, P], F32, name="s2", tag="s2", bufs=2 * max(PRE_NUM, 1) + 1)
+                s2 = work.tile([P, FT, P], F32, name="s2", tag="s2", bufs=(AHEAD + 1) * len(PRE_G) + 1)
                 nc.gpsimd.tensor_tensor(
                     out=s2[:], in0=zt[:, :, base - 2 : base - 2 + P], in1=zt[:, :, base + 2 : base + 2 + P], op=ALU.add
                 )
@@ -309,117 +349,129 @@ def tile_graphconvolutionbatch_kernel(tc, H, W, gamma, beta, out_0, out_1):
         F8t = {}
         st = {}
 
+        def piece_of(b, c, s):
+            if b == BATCH - 1 and c == NCH - 1:
+                return ((0, 2), (0, 2), (2, 3), (3, 4))[s]
+            return (0, CH)
+
         def slot(b, j):
             c = j // CH
-            if (b, c) not in Ot:
-                Ot[(b, c)] = work.tile([P, CH, FEAT], F32, name="O", tag="O")
-            return Ot[(b, c)][:, j % CH, :]
+            a, e = piece_of(b, c, j % CH)
+            if (b, c, a) not in Ot:
+                if e - a == CH:
+                    Ot[(b, c, a)] = work.tile([P, CH, FEAT], F32, name="O", tag="O")
+                else:
+                    Ot[(b, c, a)] = work.tile([P, e - a, FEAT], F32, name="OL", tag="OL")
+            return Ot[(b, c, a)][:, j % CH - a, :]
 
         def cast_vec(dst, src, n):
             t530 = work.tile([P, n], F32, name="t530", tag="t530", bufs=2)
             nc.vector.tensor_scalar_mul(out=t530[:], in0=src, scalar1=Y_SCALE)
             nc.vector.tensor_copy(out=dst, in_=t530[:], saturate=False)
 
-        def finish(b, c, a, e, first1, last1):
-            O = Ot[(b, c)]
-            nc.sync.dma_start(out=O0v[b, :, c * CH + a : c * CH + e, :], in_=O[:, a:e, :])
-            g8 = c // 2
-            if (b, g8) not in F8t:
-                F8t[(b, g8)] = work.tile([P, 2 * CH * FEAT], FP8, name="F8", tag="F8", bufs=2)
-            F8 = F8t[(b, g8)]
-            base = (c % 2) * CH * FEAT
+        def finish(b, c, a, e):
+            a0 = piece_of(b, c, a)[0]
+            O = Ot[(b, c, a0)]
+            nc.sync.dma_start(out=O0v[b, :, c * CH + a : c * CH + e, :], in_=O[:, a - a0 : e - a0, :])
+            alone = b == BATCH - 1 and c >= NCH - 2
+            if alone:
+                F8 = work.tile([P, (e - a) * FEAT], FP8, name="F8", tag="F8", bufs=4)
+                base = -a * FEAT
+            else:
+                if (b, c // 2) not in F8t:
+                    F8t[(b, c // 2)] = work.tile([P, 2 * CH * FEAT], FP8, name="F8", tag="F8", bufs=4)
+                F8 = F8t[(b, c // 2)]
+                base = (c % 2) * CH * FEAT
             for a2 in range(a, e, 2):
                 e2 = min(a2 + 2, e)
                 nc.scalar.activation(
                     out=F8[:, base + a2 * FEAT : base + e2 * FEAT],
-                    in_=O[:, a2:e2, :].rearrange("p j f -> p (j f)"),
+                    in_=O[:, a2 - a0 : e2 - a0, :].rearrange("p j f -> p (j f)"),
                     func=ACT.Copy,
                     scale=Y_SCALE,
                     saturate=False,
                 )
-            if last1 > first1:
+            if alone:
+                nc.sync.dma_start(out=O1v[b, :, (c * CH + a) * FEAT : (c * CH + e) * FEAT], in_=F8[:].bitcast(U8))
+            elif c % 2 == 1:
+                first = FEAT if c == 1 else 0
                 w8 = 2 * CH * FEAT
                 nc.sync.dma_start(
-                    out=O1v[b, :, g8 * w8 + first1 : g8 * w8 + last1], in_=F8[:, first1:last1].bitcast(U8)
+                    out=O1v[b, :, (c // 2) * w8 + first : (c // 2 + 1) * w8], in_=F8[:, first:w8].bitcast(U8)
                 )
 
         def finish_chunk(b, c):
-            lo = 1 if c == 0 else 0
-            w4 = CH * FEAT
-            if b == BATCH - 1 and c == NCH - 2:
-                finish(b, c, lo, CH, 0, w4)
-            elif c % 2 == 1:
-                finish(b, c, lo, CH, FEAT if c == 1 else 0, 2 * w4)
-            else:
-                finish(b, c, lo, CH, 0, 0)
+            finish(b, c, 1 if c == 0 else 0, CH)
 
         def seam_first_column(b):
-            Tm31 = sum_rows(zm31, Z0)
-            sm31 = keep2.tile([P, FEAT], F32, name="sm31", tag="sm31")
-            nc.scalar.activation(out=sm31[:], in_=Tm31[:], func=ACT.Copy, scale=dcol0)
+            Tmix = sum_rows(zmix[b], Z0)
+            sm0 = keep2.tile([P, FEAT], F32, name="sm0", tag="sm0")
+            nc.scalar.activation(out=sm0[:], in_=Tmix[:], func=ACT.Copy, scale=dcol31)
+            st["sm0"] = sm0
             o0 = keep2.tile([P, FEAT], F32, name="o0", tag="o0")
             nc.vector.scalar_tensor_tensor(
-                out=o0[:], in0=st["m0"][:], scalar=ratio0, in1=sm31[:], op0=ALU.mult, op1=ALU.add
+                out=o0[:], in0=Tmix[:], scalar=dcol0, in1=st["m0r"][:], op0=ALU.mult, op1=ALU.add
             )
             nc.sync.dma_start(out=O0v[b, :, 0, :], in_=o0[:])
             f80 = keep2.tile([P, FEAT], FP8, name="f80", tag="f80")
             nc.scalar.activation(out=f80[:], in_=o0[:], func=ACT.Copy, scale=Y_SCALE, saturate=False)
             nc.sync.dma_start(out=O1v[b, :, 0:FEAT], in_=f80[:].bitcast(U8))
 
-        for g in range(AHEAD):
-            make_z(g, (0, 1, 2, 3))
+        make_z(0, (0, 1, 2, 3), (2, 3))
+        edges(0)
+        pre_add(0)
+        make_z(1, (0, 1, 2, 3))
+        edges(1)
+        pre_add(1)
         for g in range(NQ):
             b, c = divmod(g, NCH)
             zt = Z[g % NZ]
             last = g == NQ - 1
-            w4 = CH * FEAT
             if c == NCH - 1:
                 seam_first_column(b)
-            for jj in range(CH):
-                j = c * CH + jj
-                if jj % 2 == 0 and g + AHEAD < NQ:
-                    make_z(g + AHEAD, (jj, jj + 1))
-                T = sum_rows(zt, Z0 + jj * WIN, pres.get((g, jj)))
-                if j % 2 == 0:
-                    st["Tev"] = T
-                    if j >= 2:
-                        nc.vector.scalar_tensor_tensor(
-                            out=slot(b, j - 1), in0=T[:], scalar=dA, in1=st["m"][:], op0=ALU.mult, op1=ALU.add
-                        )
-                        if (j - 1) % CH == CH - 1:
-                            finish_chunk(b, (j - 1) // CH)
-                        if last and jj == 2:
-                            finish(b, c, 0, 2, w4, w4 + 2 * FEAT)
-                else:
-                    S = work.tile([P, FEAT], F32, name="S", tag="S")
-                    nc.vector.tensor_scalar_mul(out=S[:], in0=T[:], scalar1=dA)
-                    if j == 1:
-                        m = keep2.tile([P, FEAT], F32, name="m0", tag="m0")
-                        st["m0"] = m
-                    else:
-                        m = work.tile([P, FEAT], F32, name="m", tag="m")
+            for half in range(2):
+                i = 2 * c + half
+                if g + AHEAD < NQ:
+                    make_z(g + AHEAD, (2 * half, 2 * half + 1))
+                T_odd = sum_rows(zt, Z0 + (2 * half + 1) * WIN, pres.get((g, 2 * half + 1)))
+                S = work.tile([P, FEAT], F32, name="S", tag="S", bufs=SMB)
+                nc.vector.tensor_scalar_mul(out=S[:], in0=T_odd[:], scalar1=dA)
+                T_even = sum_rows(zt, Z0 + 2 * half * WIN, pres.get((g, 2 * half)))
+                if i >= 1:
                     nc.vector.scalar_tensor_tensor(
-                        out=m[:], in0=st["Tev"][:], scalar=dA, in1=S[:], op0=ALU.mult, op1=ALU.add
+                        out=slot(b, 2 * i - 1), in0=T_even[:], scalar=dA, in1=st["m"][:], op0=ALU.mult, op1=ALU.add
                     )
-                    if j >= 3:
-                        if GADD and not (last and jj == 3):
-                            nc.gpsimd.tensor_tensor(out=slot(b, j - 1), in0=st["S"][:], in1=m[:], op=ALU.add)
-                        else:
-                            nc.vector.tensor_add(out=slot(b, j - 1), in0=st["S"][:], in1=m[:])
-                    st["S"] = S
-                    st["m"] = m
-            if c == 0:
-                Tm0 = sum_rows(zm0, Z0)
-                sm0 = keep2.tile([P, FEAT], F32, name="sm0", tag="sm0")
-                nc.scalar.activation(out=sm0[:], in_=Tm0[:], func=ACT.Copy, scale=dcol31)
-                st["sm0"] = sm0
-            if c == NCH - 1:
-                if last:
-                    finish(b, c, 2, 3, w4 + 2 * FEAT, w4 + 3 * FEAT)
+                m = work.tile([P, FEAT], F32, name="m", tag="m", bufs=SMB)
                 nc.vector.scalar_tensor_tensor(
-                    out=slot(b, J - 1), in0=st["m"][:], scalar=ratio31, in1=st["sm0"][:], op0=ALU.mult, op1=ALU.add
+                    out=m[:], in0=T_even[:], scalar=dA, in1=S[:], op0=ALU.mult, op1=ALU.add
                 )
-                if last:
-                    finish(b, c, 3, 4, w4 + 3 * FEAT, 2 * w4)
-                else:
-                    finish_chunk(b, c)
+                if i >= 1 and half == 0:
+                    finish_chunk(b, c - 1)
+                if last and half == 1:
+                    finish(b, c, 0, 2)
+                if i == J // 2 - 1:
+                    nc.vector.scalar_tensor_tensor(
+                        out=slot(b, J - 1), in0=m[:], scalar=ratio31, in1=st["sm0"][:], op0=ALU.mult, op1=ALU.add
+                    )
+                    if last:
+                        finish(b, c, 3, 4)
+                if i >= 1 and (last or i == J // 2 - 1):
+                    nc.vector.tensor_add(out=slot(b, 2 * i), in0=st["S"][:], in1=m[:])
+                elif i >= 1:
+                    nc.gpsimd.tensor_tensor(out=slot(b, 2 * i), in0=st["S"][:], in1=m[:], op=ALU.add)
+                if i == J // 2 - 1:
+                    if last:
+                        finish(b, c, 2, 3)
+                    else:
+                        finish_chunk(b, c)
+                if i == 0:
+                    m0r = keep2.tile([P, FEAT], F32, name="m0r", tag="m0r")
+                    nc.gpsimd.tensor_scalar(
+                        out=m0r[:], in0=m[:], scalar1=ratio0, scalar2=0.0, op0=ALU.mult, op1=ALU.add
+                    )
+                    st["m0r"] = m0r
+                st["S"] = S
+                st["m"] = m
+            if g + AHEAD < NQ:
+                edges(g + AHEAD)
+                pre_add(g + AHEAD)

@@ -32,7 +32,7 @@ PRE_NUM, PRE_DEN = 0, 4
 SC_FT = 3
 SC_Q = (1, 2, 3, 5, 6, 7, 9, 10, 11, 13)
 NE = 14
-PRE_G = (3,)
+PRE_G = (1, 3)
 
 EPS_BN = 1e-5
 EPS_DEG = 1e-5

from contextlib import ExitStack

import concourse.masks as masks
import concourse.mybir as mybir

F32 = mybir.dt.float32
BF16 = mybir.dt.bfloat16
U32 = mybir.dt.uint32
U8 = mybir.dt.uint8
FP8X4 = mybir.dt.float8_e4m3fn_x4
FP8 = mybir.dt.float8_e4m3fn
ALU = mybir.AluOpType
ACT = mybir.ActivationFunctionType

BATCH, NODES, K, FEAT = 2, 4096, 512, 512
FLOPS = 2 * BATCH * NODES * K * FEAT

P = 128
J = NODES // P
CH = 4
NCH = J // CH
NQ = BATCH * NCH
FT = FEAT // P
WIN = 130
ZW = 5 * WIN
Z0 = 4
NZ = 4
LOOK = 5
AHEAD = 2
GADD = True
PRE_NUM, PRE_DEN = 0, 4
SC_FT = 3
SC_Q = (1, 2, 3, 5, 6, 7, 9, 10, 11, 13)
NE = 14
PRE_G = (1, 3)

EPS_BN = 1e-5
EPS_DEG = 1e-5
D9 = (9.0 + EPS_DEG) ** -0.5
D6 = (6.0 + EPS_DEG) ** -0.5
D4 = (4.0 + EPS_DEG) ** -0.5
R69 = D6 / D9
R46 = D4 / D6
RC = D4 * D9 / (D6 * D6)
Y_SCALE = 530.0
VCAST = 0
SMB = 6


def tile_graphconvolutionbatch_kernel(tc, H, W, gamma, beta, out_0, out_1):
    nc = tc.nc
    with ExitStack() as ctx:
        const = ctx.enter_context(tc.tile_pool(name="const", bufs=1))
        psY = ctx.enter_context(tc.psum_pool(name="psY", bufs=4))
        psT = ctx.enter_context(tc.psum_pool(name="psT", bufs=4))

        Hv = H.rearrange("b (p j) k -> b p j k", j=J)
        O0v = out_0.rearrange("b (p j) f -> b p j f", j=J)
        O1v = out_1.rearrange("b (p j) f -> b p (j f)", j=J)

        with ExitStack() as p1:
            hpool = p1.enter_context(tc.tile_pool(name="hpool", bufs=7))
            gpool = p1.enter_context(tc.tile_pool(name="gpool", bufs=3))
            hraw = {}

            def load(q):
                b, c = divmod(q, NCH)
                t = hpool.tile([P, CH, K], BF16, name="hraw", tag="hraw")
                if q == 0:
                    for jj in range(CH):
                        nc.sync.dma_start(out=t[:, jj, :], in_=Hv[b, :, jj, :])
                else:
                    nc.sync.dma_start(out=t[:], in_=Hv[b, :, c * CH : (c + 1) * CH, :])
                hraw[q] = t

            gb = const.tile([P, P], BF16, name="gb")
            nc.vector.memset(gb[:], 0.0)
            nc.scalar.dma_start(out=gb[0:4, :], in_=gamma.rearrange("(t p) -> t p", p=P))
            nc.scalar.dma_start(out=gb[4:8, :], in_=beta.rearrange("(t p) -> t p", p=P))
            load(0)
            wraw = const.tile([P, 4, FEAT], BF16, name="wraw")
            nc.sync.dma_start(out=wraw[:], in_=W.rearrange("(p t) f -> p t f", t=4))
            for q in range(1, LOOK):
                load(q)

            identF = const.tile([P, P], F32, name="identF")
            masks.make_identity(nc, identF[:])
            identB = const.tile([P, P], BF16, name="identB")
            masks.make_identity(nc, identB[:])

            wg = const.tile([P, FEAT * 4], BF16, name="wg", align_bytes=64)
            nc.vector.tensor_copy(
                out=wg[:].rearrange("p (f t) -> p f t", t=4), in_=wraw[:].rearrange("p t f -> p f t")
            )
            wc = const.tile([P, FEAT], U32, name="wc", align_bytes=64)
            ws = const.tile([P, FEAT], U8, name="ws", align_bytes=64)
            nc.vector.quantize_mx(out=wc[:].bitcast(FP8X4), scales=ws[:], in_=wg[:])

            rt = const.tile([P, P], F32, name="rt")
            nc.gpsimd.memset(rt[:], 0.0)
            nc.gpsimd.memset(rt[0:32, 0:128:2], 1.0)
            nc.gpsimd.memset(rt[32:64, 0:128:126], 1.0)
            nc.gpsimd.memset(rt[64:96, 1:128:126], 1.0)

            Z = []
            for i in range(NZ):
                zt = const.tile([P, FT, ZW], F32, name="z%d" % i)
                nc.gpsimd.memset(zt[:].rearrange("p f (r c) -> p f r c", c=WIN)[:, :, :, 0:6], 0.0)
                Z.append(zt)
            zmix = []
            for i in range(BATCH):
                zx = const.tile([P, FT, 136], F32, name="zmix%d" % i)
                nc.gpsimd.memset(zx[:], 0.0)
                zmix.append(zx)
            neghalf = const.tile([P, FT], F32, name="neghalf")
            nc.gpsimd.memset(neghalf[:], -0.5)

            gbT = const.tile([P, 8], F32, name="gbT")
            gb9 = const.tile([P, 8], F32, name="gb9")
            msk = const.tile([P, 8], F32, name="msk")
            tab = const.tile([P, 8], F32, name="tab")
            dA = tab[:, 0:1]
            ratio0 = tab[:, 1:2]
            ratio31 = tab[:, 2:3]
            dcol0 = tab[:, 3:4]
            dcol31 = tab[:, 4:5]

            def small_tables():
                gb_ps = psT.tile([P, P], BF16, name="gb_ps", tag="t")
                nc.tensor.transpose(out=gb_ps[:], in_=gb[:], identity=identB[:])
                nc.vector.tensor_copy(out=gbT[:], in_=gb_ps[:, 0:8])
                nc.vector.tensor_scalar_mul(out=gb9[:], in0=gbT[:], scalar1=D9)
                tab_ps = psT.tile([P, P], F32, name="tab_ps", tag="t")
                nc.tensor.transpose(out=tab_ps[:], in_=rt[:], identity=identF[:])
                nc.vector.tensor_copy(out=msk[:, 0:3], in_=tab_ps[:, 0:96:32])
                m_even = msk[:, 0:1]
                m_c0 = msk[:, 1:2]
                m_c1 = msk[:, 2:3]
                nc.vector.tensor_add(out=msk[:, 3:4], in0=m_c0, in1=m_c1)
                nc.vector.tensor_scalar(out=dA, in0=msk[:, 3:4], scalar1=D6 - D9, scalar2=D9, op0=ALU.mult, op1=ALU.add)
                nc.vector.tensor_scalar(out=msk[:, 4:5], in0=m_even, scalar1=R69 - 1.0, scalar2=1.0, op0=ALU.mult, op1=ALU.add)
                nc.vector.tensor_scalar(out=msk[:, 5:6], in0=m_even, scalar1=1.0 - R69, scalar2=R69, op0=ALU.mult, op1=ALU.add)
                nc.vector.scalar_tensor_tensor(out=ratio0, in0=m_c0, scalar=R46 - R69, in1=msk[:, 4:5], op0=ALU.mult, op1=ALU.add)
                nc.vector.scalar_tensor_tensor(out=ratio31, in0=m_c1, scalar=R46 - R69, in1=msk[:, 5:6], op0=ALU.mult, op1=ALU.add)
                nc.vector.tensor_scalar_mul(out=tab[:, 5:7], in0=tab[:, 1:3], scalar1=dA)
                nc.vector.tensor_scalar(out=msk[:, 6:7], in0=m_even, scalar1=-1.0, scalar2=1.0, op0=ALU.mult, op1=ALU.add)
                nc.vector.tensor_mul(out=dcol0, in0=tab[:, 5:6], in1=msk[:, 6:7])
                nc.vector.tensor_mul(out=dcol31, in0=tab[:, 6:7], in1=m_even)

            ctx.enter_context(tc.manual_schedule(engines={mybir.EngineType.PE}))

            NL = NQ - NE
            statsE = const.tile([P, FT, NE + 1, 6], F32, name="statsE")
            statsL = const.tile([P, FT, 3 + 6 * NL], F32, name="statsL")
            nc.vector.memset(statsL[:, :, 0:1], 512.0 * NE)
            pm = const.tile([P, FT, 2], F32, name="pm")
            tot = const.tile([P, 2], F32, name="tot")
            dm = const.tile([P, 2], F32, name="dm")
            sums = const.tile([P, 2, NQ], F32, name="sums")
            negc = const.tile([P, 1], F32, name="negc")
            nslot = {}
            ycp = {}
            grouped = {}
            hc = {}
            hs = {}

            def flip(q):
                G = gpool.tile([P, CH * P * 4], BF16, name="G", tag="G", align_bytes=64)
                Gw = G[:].bitcast(F32)
                for h in range(2):
                    xt = psT.tile([P, 512], F32, name="xt", tag="t")
                    for jl in range(2):
                        words = hraw[q][:, 2 * h + jl, :].bitcast(F32)
                        for u in range(2):
                            s = 2 * jl + u
                            nc.tensor.transpose(
                                out=xt[:, s * P : (s + 1) * P], in_=words[:, u:256:2], identity=identF[:]
                            )
                    nc.scalar.copy(
                        out=Gw[:, h * 512 : (h + 1) * 512].rearrange("p (j r u) -> p j r u", j=2, u=2),
                        in_=xt[:].rearrange("p (j u r) -> p j r u", j=2, u=2),
                    )
                grouped[q] = G

            def quant(q):
                c_t = const.tile([P, 512], U32, name="hc%d" % q, align_bytes=64)
                s_t = const.tile([P, 512], U8, name="hs%d" % q, align_bytes=64)
                nc.vector.quantize_mx(out=c_t[:].bitcast(FP8X4), scales=s_t[:], in_=grouped[q][:])
                hc[q] = c_t
                hs[q] = s_t

            def mult(q, ft):
                Y = psY.tile([P, 512], F32, name="Y", tag="y")
                nc.tensor.matmul_mx(
                    out=Y[:],
                    lhsT=wc[:, ft * P : (ft + 1) * P].bitcast(FP8X4),
                    lhsT_scale=ws[:, ft * P : (ft + 1) * P],
                    rhs=hc[q][:].bitcast(FP8X4),
                    rhs_scale=hs[q][:],
                    start=True,
                    stop=True,
                )
                return Y

            def mm_stats(q):
                for ft in range(FT):
                    Y = mult(q, ft)
                    if ft == SC_FT and q in SC_Q:
                        i = SC_Q.index(q)
                        yc = const.tile([P, 512], F32, name="ycp%d" % q)
                        ycp[q] = yc
                        nc.scalar.activation(out=yc[:], in_=Y[:], func=ACT.Identity, accum_out=sums[:, 0, i : i + 1])
                        if i == 0:
                            nc.vector.tensor_scalar_mul(out=negc[:], in0=sums[:, 0, 0:1], scalar1=-1.0 / 512.0)
                        junk2 = gpool.tile([P, 512], F32, name="junk2", tag="junk", bufs=2)
                        nc.scalar.activation(
                            out=junk2[:], in_=Y[:], func=ACT.Square, bias=negc[:, 0:1], accum_out=sums[:, 1, i : i + 1]
                        )
                    elif q < NE:
                        s = nslot.get(ft, 0)
                        nslot[ft] = s + 1
                        nc.vector.bn_stats(out=statsE[:, ft, s, :], in_=Y[:])
                    else:
                        o = 3 + 6 * (q - NE)
                        nc.vector.bn_stats(out=statsL[:, ft, o : o + 6], in_=Y[:])

            def early_aggr():
                n_sc = 512.0 * len(SC_Q)
                nc.vector.tensor_reduce(out=tot[:], in_=sums[:, :, 0 : len(SC_Q)], axis=mybir.AxisListType.X, op=ALU.add)
                ent = statsE[:, SC_FT, nslot[SC_FT], 0:3]
                nc.vector.memset(ent[:, 0:1], n_sc)
                nc.vector.tensor_scalar_mul(out=ent[:, 1:2], in0=tot[:, 0:1], scalar1=1.0 / n_sc)
                nc.vector.tensor_add(out=dm[:, 0:1], in0=ent[:, 1:2], in1=negc[:])
                nc.vector.tensor_mul(out=dm[:, 1:2], in0=dm[:, 0:1], in1=dm[:, 0:1])
                nc.vector.scalar_tensor_tensor(
                    out=ent[:, 2:3], in0=dm[:, 1:2], scalar=-n_sc, in1=tot[:, 1:2], op0=ALU.mult, op1=ALU.add
                )
                for ft in range(FT):
                    n_el = 6 * nslot[ft] + (3 if ft == SC_FT else 0)
                    nc.vector.bn_aggr(out=pm[:, ft, :], in_=statsE[:, ft, :, :].rearrange("p c s -> p (c s)")[:, 0:n_el])
                nc.vector.tensor_copy(out=statsL[:, :, 1:2], in_=pm[:, :, 0:1])
                nc.vector.tensor_scalar_mul(out=statsL[:, :, 2:3], in0=pm[:, :, 1:2], scalar1=512.0 * NE)

            for step in range(NQ + 2):
                if step + LOOK < NQ:
                    load(step + LOOK)
                if step < NQ:
                    flip(step)
                if 1 <= step <= NQ:
                    quant(step - 1)
                if step >= 2:
                    mm_stats(step - 2)
                if step == 4:
                    small_tables()
                if step == NE + 1:
                    early_aggr()

        mv = const.tile([P, FT, 2], F32, name="mv")
        for ft in range(FT):
            nc.vector.bn_aggr(out=mv[:, ft, :], in_=statsL[:, ft, :])
        ve = const.tile([P, FT], F32, name="ve")
        nc.vector.tensor_scalar_add(out=ve[:], in0=mv[:, :, 1], scalar1=EPS_BN)
        rstd = const.tile([P, FT], F32, name="rstd")
        nc.gpsimd.tensor_tensor(out=rstd[:], in0=ve[:], in1=neghalf[:], op=ALU.pow)
        ab9 = const.tile([P, 2, FT], F32, name="ab9")
        nc.vector.tensor_mul(out=ab9[:, 0, :], in0=gb9[:, 0:4], in1=rstd[:])
        ma = const.tile([P, FT], F32, name="ma")
        nc.vector.tensor_mul(out=ma[:], in0=mv[:, :, 0], in1=ab9[:, 0, :])
        nc.vector.tensor_sub(out=ab9[:, 1, :], in0=gb9[:, 4:8], in1=ma[:])

        work = ctx.enter_context(tc.tile_pool(name="work", bufs=3))
        keep2 = ctx.enter_context(tc.tile_pool(name="keep2", bufs=2))
        def scale_cols(view, factor):
            nc.gpsimd.tensor_scalar(
                out=view, in0=view, scalar1=factor, scalar2=0.0, op0=ALU.mult, op1=ALU.add
            )

        def make_z(g, fts, vec_fts=()):
            c = g % NCH
            zt = Z[g % NZ]
            for ft in fts:
                Y = ycp[g] if ft == SC_FT and g in SC_Q else mult(g, ft)
                z_out = zt[:, ft, Z0 : Z0 + CH * WIN].rearrange("p (w c) -> p w c", c=WIN)[:, :, 0:P]
                y_in = Y[:].rearrange("p (w c) -> p w c", c=P)
                if ft in vec_fts:
                    nc.vector.tensor_scalar(
                        out=z_out,
                        in0=y_in,
                        scalar1=ab9[:, 0, ft : ft + 1],
                        scalar2=ab9[:, 1, ft : ft + 1],
                        op0=ALU.mult,
                        op1=ALU.add,
                    )
                    nc.vector.tensor_scalar_max(out=z_out, in0=z_out, scalar1=0.0)
                else:
                    nc.scalar.activation(
                        out=z_out,
                        in_=y_in,
                        func=ACT.Relu,
                        bias=ab9[:, 1, ft : ft + 1],
                        scale=ab9[:, 0, ft : ft + 1],
                    )

        def edges(g):
            c = g % NCH
            zt = Z[g % NZ]
            scale_cols(zt[:].rearrange("p f (r c) -> p f r c", c=WIN)[:, :, :, 0:6], R69)
            if c == 0:
                scale_cols(zt[:, :, Z0 : Z0 + P : 2], R69)
                scale_cols(zt[:, :, Z0 : Z0 + P : 126], RC)
                nc.gpsimd.tensor_copy(out=zmix[g // NCH][:, :, Z0 : Z0 + P : 2], in_=zt[:, :, Z0 + 1 : Z0 + P : 2])
            if c == NCH - 1:
                w3 = Z0 + 3 * WIN
                scale_cols(zt[:, :, w3 + 1 : w3 + P : 2], R69)
                scale_cols(zt[:, :, w3 + 1 : w3 + P : 126], RC)
                nc.gpsimd.tensor_copy(out=zmix[g // NCH][:, :, Z0 + 1 : Z0 + P : 2], in_=zt[:, :, w3 : w3 + P : 2])

        def sum_rows(src, base, pre=None):
            T = psT.tile([P, 512], F32, name="T", tag="t")
            for ft in range(FT):
                if pre is None:
                    wins = [src[:, ft, base + 2 * (w - 1) : base + 2 * (w - 1) + P] for w in range(3)]
                else:
                    wins = [src[:, ft, base : base + P], pre[:, ft, :]]
                for w in range(len(wins)):
                    nc.tensor.matmul(
                        out=T[:, ft * P : (ft + 1) * P],
                        lhsT=wins[w],
                        rhs=identF[:],
                        is_transpose=True,
                        start=(w == 0),
                        stop=(w == len(wins) - 1),
                    )
            return T

        pres = {}

        def pre_add(g):
            zt = Z[g % NZ]
            for jj in PRE_G:
                base = Z0 + jj * WIN
                s2 = work.tile([P, FT, P], F32, name="s2", tag="s2", bufs=(AHEAD + 1) * len(PRE_G) + 1)
                nc.gpsimd.tensor_tensor(
                    out=s2[:], in0=zt[:, :, base - 2 : base - 2 + P], in1=zt[:, :, base + 2 : base + 2 + P], op=ALU.add
                )
                pres[(g, jj)] = s2

        Ot = {}
        F8t = {}
        st = {}

        def piece_of(b, c, s):
            if b == BATCH - 1 and c == NCH - 1:
                return ((0, 2), (0, 2), (2, 3), (3, 4))[s]
            return (0, CH)

        def slot(b, j):
            c = j // CH
            a, e = piece_of(b, c, j % CH)
            if (b, c, a) not in Ot:
                if e - a == CH:
                    Ot[(b, c, a)] = work.tile([P, CH, FEAT], F32, name="O", tag="O")
                else:
                    Ot[(b, c, a)] = work.tile([P, e - a, FEAT], F32, name="OL", tag="OL")
            return Ot[(b, c, a)][:, j % CH - a, :]

        def cast_vec(dst, src, n):
            t530 = work.tile([P, n], F32, name="t530", tag="t530", bufs=2)
            nc.vector.tensor_scalar_mul(out=t530[:], in0=src, scalar1=Y_SCALE)
            nc.vector.tensor_copy(out=dst, in_=t530[:], saturate=False)

        def finish(b, c, a, e):
            a0 = piece_of(b, c, a)[0]
            O = Ot[(b, c, a0)]
            nc.sync.dma_start(out=O0v[b, :, c * CH + a : c * CH + e, :], in_=O[:, a - a0 : e - a0, :])
            alone = b == BATCH - 1 and c >= NCH - 2
            if alone:
                F8 = work.tile([P, (e - a) * FEAT], FP8, name="F8", tag="F8", bufs=4)
                base = -a * FEAT
            else:
                if (b, c // 2) not in F8t:
                    F8t[(b, c // 2)] = work.tile([P, 2 * CH * FEAT], FP8, name="F8", tag="F8", bufs=4)
                F8 = F8t[(b, c // 2)]
                base = (c % 2) * CH * FEAT
            for a2 in range(a, e, 2):
                e2 = min(a2 + 2, e)
                nc.scalar.activation(
                    out=F8[:, base + a2 * FEAT : base + e2 * FEAT],
                    in_=O[:, a2 - a0 : e2 - a0, :].rearrange("p j f -> p (j f)"),
                    func=ACT.Copy,
                    scale=Y_SCALE,
                    saturate=False,
                )
            if alone:
                nc.sync.dma_start(out=O1v[b, :, (c * CH + a) * FEAT : (c * CH + e) * FEAT], in_=F8[:].bitcast(U8))
            elif c % 2 == 1:
                first = FEAT if c == 1 else 0
                w8 = 2 * CH * FEAT
                nc.sync.dma_start(
                    out=O1v[b, :, (c // 2) * w8 + first : (c // 2 + 1) * w8], in_=F8[:, first:w8].bitcast(U8)
                )

        def finish_chunk(b, c):
            finish(b, c, 1 if c == 0 else 0, CH)

        def seam_first_column(b):
            Tmix = sum_rows(zmix[b], Z0)
            sm0 = keep2.tile([P, FEAT], F32, name="sm0", tag="sm0")
            nc.scalar.activation(out=sm0[:], in_=Tmix[:], func=ACT.Copy, scale=dcol31)
            st["sm0"] = sm0
            o0 = keep2.tile([P, FEAT], F32, name="o0", tag="o0")
            nc.vector.scalar_tensor_tensor(
                out=o0[:], in0=Tmix[:], scalar=dcol0, in1=st["m0r"][:], op0=ALU.mult, op1=ALU.add
            )
            nc.sync.dma_start(out=O0v[b, :, 0, :], in_=o0[:])
            f80 = keep2.tile([P, FEAT], FP8, name="f80", tag="f80")
            nc.scalar.activation(out=f80[:], in_=o0[:], func=ACT.Copy, scale=Y_SCALE, saturate=False)
            nc.sync.dma_start(out=O1v[b, :, 0:FEAT], in_=f80[:].bitcast(U8))

        make_z(0, (0, 1, 2, 3), (2, 3))
        edges(0)
        pre_add(0)
        make_z(1, (0, 1, 2, 3))
        edges(1)
        pre_add(1)
        for g in range(NQ):
            b, c = divmod(g, NCH)
            zt = Z[g % NZ]
            last = g == NQ - 1
            if c == NCH - 1:
                seam_first_column(b)
            for half in range(2):
                i = 2 * c + half
                if g + AHEAD < NQ:
                    make_z(g + AHEAD, (2 * half, 2 * half + 1))
                T_odd = sum_rows(zt, Z0 + (2 * half + 1) * WIN, pres.get((g, 2 * half + 1)))
                S = work.tile([P, FEAT], F32, name="S", tag="S", bufs=SMB)
                nc.vector.tensor_scalar_mul(out=S[:], in0=T_odd[:], scalar1=dA)
                T_even = sum_rows(zt, Z0 + 2 * half * WIN, pres.get((g, 2 * half)))
                if i >= 1:
                    nc.vector.scalar_tensor_tensor(
                        out=slot(b, 2 * i - 1), in0=T_even[:], scalar=dA, in1=st["m"][:], op0=ALU.mult, op1=ALU.add
                    )
                m = work.tile([P, FEAT], F32, name="m", tag="m", bufs=SMB)
                nc.vector.scalar_tensor_tensor(
                    out=m[:], in0=T_even[:], scalar=dA, in1=S[:], op0=ALU.mult, op1=ALU.add
                )
                if i >= 1 and half == 0:
                    finish_chunk(b, c - 1)
                if last and half == 1:
                    finish(b, c, 0, 2)
                if i == J // 2 - 1:
                    nc.vector.scalar_tensor_tensor(
                        out=slot(b, J - 1), in0=m[:], scalar=ratio31, in1=st["sm0"][:], op0=ALU.mult, op1=ALU.add
                    )
                    if last:
                        finish(b, c, 3, 4)
                if i >= 1 and (last or i == J // 2 - 1):
                    nc.vector.tensor_add(out=slot(b, 2 * i), in0=st["S"][:], in1=m[:])
                elif i >= 1:
                    nc.gpsimd.tensor_tensor(out=slot(b, 2 * i), in0=st["S"][:], in1=m[:], op=ALU.add)
                if i == J // 2 - 1:
                    if last:
                        finish(b, c, 2, 3)
                    else:
                        finish_chunk(b, c)
                if i == 0:
                    m0r = keep2.tile([P, FEAT], F32, name="m0r", tag="m0r")
                    nc.gpsimd.tensor_scalar(
                        out=m0r[:], in0=m[:], scalar1=ratio0, scalar2=0.0, op0=ALU.mult, op1=ALU.add
                    )
                    st["m0r"] = m0r
                st["S"] = S
                st["m"] = m
            if g + AHEAD < NQ:
                edges(g + AHEAD)
                pre_add(g + AHEAD)
